import numpy as np
import ml_dtypes


def mxq(x, axis, fmt="e4m3"):
    dtype, down = {"e4m3": (ml_dtypes.float8_e4m3fn, 7), "e5m2": (ml_dtypes.float8_e5m2, 14)}[fmt]
    v = np.moveaxis(np.asarray(x, np.float32).astype(ml_dtypes.bfloat16).astype(np.float64), axis, -1)
    blocks = v.reshape(v.shape[:-1] + (-1, 32))
    amax = np.abs(blocks).max(-1, keepdims=True)
    byte = np.maximum(np.where(amax > 0, np.frexp(amax)[1] - 1 + 127, 0) - down, 1)
    scale = np.exp2(byte - 127.0)
    codes = (blocks / scale).astype(np.float32).astype(dtype).astype(np.float64)
    return np.moveaxis((codes * scale).reshape(v.shape), -1, axis)


WIDE = False


def mx_kscale(k):
    if not WIDE:
        return np.ones(k)
    levels = np.array([10, -10, 5, -5, 0])
    if k % 512:
        return np.exp2(np.random.permutation(np.resize(levels, k // 32))).repeat(32)
    a = np.empty((k // 512, 16))
    for p in range(k // 512):
        a[p, :8] = np.random.permutation(np.resize(levels, 8))
        for g in range(8):
            far = levels[np.abs(levels - a[p, g]) >= 10]
            a[p, g + 8] = far[np.random.randint(len(far))]
    return np.exp2(a.ravel()).repeat(32)


BF16 = ml_dtypes.bfloat16


def bf(x):
    return np.asarray(x, np.float32).astype(BF16)


def f64(x):
    return np.asarray(x).astype(np.float64)


H, D_CONTENT, D_POS, D_K, D_V, B, L = 16, 512, 128, 128, 128, 8, 512
D_MODEL = D_CONTENT + D_POS
T = B * L
DV1 = D_V // 2
KP = H * DV1
EPS = 1e-3


def setup_inputs():
    s1, s2 = mx_kscale(KP), mx_kscale(KP)
    sc = np.concatenate([s1.reshape(H, DV1), s2.reshape(H, DV1)], axis=1)
    return {
        "attn_out": bf(np.random.standard_normal((H, B, L, D_V)) * 0.4 * sc[:, None, None, :]),
        "inp": bf(np.random.standard_normal((T, D_MODEL)) * 0.05 + np.random.standard_normal((T, 1)) * 0.03),
        "w_proj1": bf(np.random.standard_normal((KP, D_CONTENT)) * 0.1 / np.sqrt(KP) / s1[:, None]),
        "w_proj2": bf(np.random.standard_normal((KP, D_POS)) * 0.1 / np.sqrt(KP) / s2[:, None]),
        "ln_a": bf(1.0 + 0.1 * np.random.standard_normal(D_MODEL)),
        "ln_b": bf(0.1 * np.random.standard_normal(D_MODEL)),
    }


def reference(attn_out, inp, w_proj1, w_proj2, ln_a, ln_b):
    o = f64(attn_out).reshape(H, T, D_V).transpose(1, 0, 2)
    o1 = o[:, :, :DV1].reshape(T, KP)
    o2 = o[:, :, DV1:].reshape(T, KP)
    y1 = mxq(o1, 1, "e4m3") @ mxq(f64(w_proj1), 0, "e4m3")
    y2 = mxq(o2, 1, "e4m3") @ mxq(f64(w_proj2), 0, "e4m3")
    z = np.concatenate([y1, y2], -1) + f64(inp)
    mu = np.mean(z, axis=-1, keepdims=True)
    sigma = np.std(z, axis=-1, keepdims=True, ddof=1)
    ln = (z - mu) / (sigma + EPS)
    return ln * f64(ln_a) + f64(ln_b)

@@ -1,0 +1,311 @@
+from contextlib import ExitStack
+
+import concourse.mybir as mybir
+from concourse.masks import make_identity
+
+BF16 = mybir.dt.bfloat16
+F32 = mybir.dt.float32
+I32 = mybir.dt.int32
+U32 = mybir.dt.uint32
+U8 = mybir.dt.uint8
+FP8X4 = mybir.dt.float8_e4m3fn_x4
+ALU = mybir.AluOpType
+ACT = mybir.ActivationFunctionType
+
+P = 128
+PACK = 4
+HEADS = 16
+TOKENS = 4096
+D_V = 128
+D_CONTENT = 512
+D_POS = 128
+D_MODEL = D_CONTENT + D_POS
+EPS = 1e-3
+
+N_TILES = TOKENS // P
+QUADS = 4
+HEADS_IN_QUAD = HEADS // QUADS
+HALF_ROWS = 16
+HEAD_ROWS = 2 * HALF_ROWS
+WORDS = HEADS * D_V // 2
+QUAD_WORDS = WORDS // QUADS
+BANKS = 2
+ROUND = 2
+N_ROUNDS = N_TILES // ROUND
+CHUNK = 4
+N_CHUNKS = N_TILES // CHUNK
+ROUNDS_PER_CHUNK = CHUNK // ROUND
+CHUNKS_AHEAD = 2
+
+FLOPS = 2 * TOKENS * (HEADS * D_V // 2) * D_MODEL
+
+
+def tile_multiheadattention_pa_t_kernel(tc, attn_out, inp, w_proj1, w_proj2, ln_a, ln_b, out):
+    nc = tc.nc
+    x_view = attn_out.rearrange("h b l f -> h (b l) f").rearrange("h (m k) f -> k m h f", k=N_TILES)
+    inp_view = inp.rearrange("(m k) c -> m k c", k=N_TILES)
+    out_view = out.rearrange("(m k) c -> m k c", k=N_TILES)
+
+    with ExitStack() as ctx:
+        ctx.enter_context(tc.manual_schedule())
+        const = ctx.enter_context(tc.tile_pool(name="const", bufs=1))
+        xin = ctx.enter_context(tc.tile_pool(name="xin", bufs=3))
+        resin = ctx.enter_context(tc.tile_pool(name="resin", bufs=3))
+        grouped = ctx.enter_context(tc.tile_pool(name="grouped", bufs=3 * ROUND))
+        packed = ctx.enter_context(tc.tile_pool(name="packed", bufs=2 * ROUND))
+        zpool = ctx.enter_context(tc.tile_pool(name="zpool", bufs=2 * ROUND))
+        upool = ctx.enter_context(tc.tile_pool(name="upool", bufs=3 * ROUND))
+        scratch = ctx.enter_context(tc.tile_pool(name="scratch", bufs=2))
+        stats = ctx.enter_context(tc.tile_pool(name="stats", bufs=8))
+        result = ctx.enter_context(tc.tile_pool(name="result", bufs=3))
+        t_psum = ctx.enter_context(tc.psum_pool(name="t_psum", bufs=BANKS * ROUND))
+        y1_psum = ctx.enter_context(tc.psum_pool(name="y1_psum", bufs=ROUND))
+        y2_psum = ctx.enter_context(tc.psum_pool(name="y2_psum", bufs=2))
+
+        x_tiles = {}
+        res_tiles = {}
+
+        def load_x(c):
+            k0 = c * CHUNK
+            x = xin.tile([P, CHUNK, HEADS, D_V], BF16)
+            for j in range(CHUNK):
+                nc.sync.dma_start(out=x[:, j], in_=x_view[k0 + j])
+            x_tiles[c] = x
+
+        def load_residual(c):
+            k0 = c * CHUNK
+            res = resin.tile([P, CHUNK, D_MODEL], BF16)
+            nc.sync.dma_start(out=res[:], in_=inp_view[:, k0 : k0 + CHUNK, :])
+            res_tiles[c] = res
+
+        ln_rows = const.tile([P, 2, D_MODEL], BF16)
+        w1_raw = const.tile([P, QUADS, PACK, D_CONTENT], BF16)
+        w2_raw = const.tile([P, QUADS, PACK, D_POS], BF16)
+        ident = const.tile([P, P], F32)
+        make_identity(nc, ident[:])
+        nc.vector.memset(ln_rows[:].rearrange("p a n -> p (a n)").bitcast(I32), 0)
+        nc.vector.memset(w2_raw[:].rearrange("p q t n -> p (q t n)").bitcast(I32), 0)
+        nc.vector.memset(w1_raw[:].rearrange("p q t n -> p (q t n)").bitcast(I32), 0)
+        load_x(0)
+        nc.sync.dma_start(out=ln_rows[0:1, 0, :], in_=ln_a.unsqueeze(0))
+        nc.sync.dma_start(out=ln_rows[0:1, 1, :], in_=ln_b.unsqueeze(0))
+        w1_view = w_proj1.rearrange("(q h j t) n -> h j q (t n)", q=QUADS, h=HEADS_IN_QUAD, t=PACK)
+        w2_view = w_proj2.rearrange("(q h j t) n -> h j q (t n)", q=QUADS, h=HEADS_IN_QUAD, t=PACK)
+        for h in range(HEADS_IN_QUAD):
+            p0 = h * HEAD_ROWS
+            nc.sync.dma_start(
+                out=w2_raw[p0 + HALF_ROWS : p0 + HEAD_ROWS].rearrange("p q t n -> p q (t n)"), in_=w2_view[h]
+            )
+        for h in range(HEADS_IN_QUAD):
+            p0 = h * HEAD_ROWS
+            nc.sync.dma_start(out=w1_raw[p0 : p0 + HALF_ROWS].rearrange("p q t n -> p q (t n)"), in_=w1_view[h])
+        load_x(1)
+
+        ones = const.tile([P, P], BF16)
+        nc.vector.memset(ones[:], 1.0)
+        warm = const.tile([P, 1], F32)
+        nc.vector.memset(warm[:], 1.0)
+        warm_out = const.tile([P, 1], F32)
+        nc.scalar.activation(out=warm_out[:], in_=warm[:], func=ACT.Sqrt)
+
+        w1_grouped = const.tile([P, QUADS, D_CONTENT, PACK], BF16, align_bytes=64)
+        w2_grouped = const.tile([P, QUADS, D_POS, PACK], BF16, align_bytes=64)
+
+        gain_bank = y1_psum.tile([P, D_CONTENT], F32, tag="y1")
+        nc.tensor.matmul(out=gain_bank[:], lhsT=ones[:], rhs=ln_rows[:, 0, 0:D_CONTENT], start=True, stop=True)
+        shift_bank = y1_psum.tile([P, D_CONTENT], F32, tag="y1")
+        nc.tensor.matmul(out=shift_bank[:], lhsT=ones[:], rhs=ln_rows[:, 1, 0:D_CONTENT], start=True, stop=True)
+        tails_bank = y2_psum.tile([P, 2, D_POS], F32, tag="y2")
+        nc.tensor.matmul(out=tails_bank[:], lhsT=ones[:], rhs=ln_rows[:, :, D_CONTENT:D_MODEL], start=True, stop=True)
+        gain = const.tile([P, D_MODEL], F32)
+        shift = const.tile([P, D_MODEL], F32)
+        nc.scalar.copy(out=gain[:, 0:D_CONTENT], in_=gain_bank[:])
+        nc.scalar.copy(out=shift[:, 0:D_CONTENT], in_=shift_bank[:])
+        nc.scalar.copy(out=gain[:, D_CONTENT:D_MODEL], in_=tails_bank[:, 0, :])
+        nc.scalar.copy(out=shift[:, D_CONTENT:D_MODEL], in_=tails_bank[:, 1, :])
+
+        w1_codes = const.tile([P, QUADS, D_CONTENT], U32, align_bytes=64)
+        w1_scales = const.tile([P, QUADS, D_CONTENT], U8, align_bytes=64)
+        w2_codes = const.tile([P, QUADS, D_POS], U32, align_bytes=64)
+        w2_scales = const.tile([P, QUADS, D_POS], U8, align_bytes=64)
+        for q in range(QUADS):
+            nc.scalar.copy(out=w2_grouped[:, q], in_=w2_raw[:, q].rearrange("p t n -> p n t"))
+        nc.vector.quantize_mx(
+            out=w2_codes[:].rearrange("p q n -> p (q n)").bitcast(FP8X4),
+            scales=w2_scales[:].rearrange("p q n -> p (q n)"),
+            in_=w2_grouped[:].rearrange("p q n t -> p (q n t)"),
+        )
+
+        def quantise_w1(q):
+            nc.vector.quantize_mx(
+                out=w1_codes[:, q, :].bitcast(FP8X4),
+                scales=w1_scales[:, q, :],
+                in_=w1_grouped[:, q].rearrange("p n t -> p (n t)"),
+            )
+
+        for q in range(QUADS):
+            nc.vector.tensor_copy(out=w1_grouped[:, q], in_=w1_raw[:, q].rearrange("p t n -> p n t"))
+            if q > 0:
+                quantise_w1(q - 1)
+        quantise_w1(QUADS - 1)
+
+        xg_tiles = {}
+        code_tiles = {}
+        y1_tiles = {}
+        y2_tiles = {}
+        z_tiles = {}
+        sums_tiles = {}
+        mean_tiles = {}
+        u_tiles = {}
+        sigma_tiles = {}
+        inv_tiles = {}
+
+        def tiles_of(rnd):
+            return range(rnd * ROUND, (rnd + 1) * ROUND)
+
+        def transpose_round(rnd):
+            for k in tiles_of(rnd):
+                xg = grouped.tile([P, QUADS, P, PACK], BF16, align_bytes=64)
+                xg_tiles[k] = xg
+                words = x_tiles[k // CHUNK][:, k % CHUNK].rearrange("p h f -> p (h f)").bitcast(F32)
+                xg_words = xg[:].rearrange("p q m t -> p (q m t)").bitcast(F32).rearrange(
+                    "p (b q m u) -> p b q m u", b=BANKS, m=P, u=2
+                )
+                for b in range(BANKS):
+                    bank = t_psum.tile([P, QUADS // BANKS, 2, P], F32)
+                    for i in range(QUADS // BANKS):
+                        w0 = (b * (QUADS // BANKS) + i) * QUAD_WORDS
+                        for u in range(2):
+                            nc.tensor.transpose(bank[:, i, u, :], words[:, w0 + u : w0 + QUAD_WORDS : 2], ident[:])
+                    nc.scalar.copy(out=xg_words[:, b], in_=bank[:].rearrange("p q u m -> p q m u"))
+
+        def quantise(k):
+            codes = packed.tile([P, QUADS, P], U32, align_bytes=64)
+            scales = packed.tile([P, QUADS, P], U8, align_bytes=64)
+            nc.vector.quantize_mx(
+                out=codes[:].rearrange("p q m -> p (q m)").bitcast(FP8X4),
+                scales=scales[:].rearrange("p q m -> p (q m)"),
+                in_=xg_tiles[k][:].rearrange("p q m t -> p (q m t)"),
+            )
+            code_tiles[k] = (codes, scales)
+
+        def multiply_round(rnd):
+            y2 = y2_psum.tile([P, ROUND, D_POS], F32, tag="y2")
+            y2_tiles[rnd] = y2
+            for k in tiles_of(rnd):
+                codes, scales = code_tiles[k]
+                y1 = y1_psum.tile([P, D_CONTENT], F32, tag="y1")
+                for q in range(QUADS):
+                    nc.tensor.matmul_mx(
+                        out=y1[:],
+                        lhsT=codes[:, q, :].bitcast(FP8X4),
+                        lhsT_scale=scales[:, q, :],
+                        rhs=w1_codes[:, q, :].bitcast(FP8X4),
+                        rhs_scale=w1_scales[:, q, :],
+                        start=(q == 0),
+                        stop=(q == QUADS - 1),
+                    )
+                for q in range(QUADS):
+                    nc.tensor.matmul_mx(
+                        out=y2[:, k % ROUND, :],
+                        lhsT=codes[:, q, :].bitcast(FP8X4),
+                        lhsT_scale=scales[:, q, :],
+                        rhs=w2_codes[:, q, :].bitcast(FP8X4),
+                        rhs_scale=w2_scales[:, q, :],
+                        start=(q == 0),
+                        stop=(q == QUADS - 1),
+                    )
+                y1_tiles[k] = y1
+
+        def add_residual(k):
+            res = res_tiles[k // CHUNK]
+            z = zpool.tile([P, D_MODEL], F32)
+            sums = stats.tile([P, 2], F32)
+            nc.vector.scalar_tensor_tensor(
+                out=z[:, 0:D_CONTENT], in0=y1_tiles[k][:], scalar=1.0, in1=res[:, k % CHUNK, 0:D_CONTENT],
+                op0=ALU.mult, op1=ALU.add, accum_out=sums[:, 0:1],
+            )
+            nc.vector.scalar_tensor_tensor(
+                out=z[:, D_CONTENT:D_MODEL], in0=y2_tiles[k // ROUND][:, k % ROUND, :], scalar=1.0,
+                in1=res[:, k % CHUNK, D_CONTENT:D_MODEL],
+                op0=ALU.mult, op1=ALU.add, accum_out=sums[:, 1:2],
+            )
+            z_tiles[k] = z
+            sums_tiles[k] = sums
+
+        def mean(k):
+            scaled_sums = stats.tile([P, 2], F32)
+            neg_mean = stats.tile([P, 1], F32)
+            nc.scalar.activation(
+                out=scaled_sums[:], in_=sums_tiles[k][:], func=ACT.Copy, scale=-1.0 / D_MODEL, accum_out=neg_mean[:, 0:1],
+            )
+            mean_tiles[k] = neg_mean
+
+        def centre_and_gain(k):
+            u = upool.tile([P, D_MODEL], F32)
+            nc.vector.scalar_tensor_tensor(
+                out=u[:], in0=z_tiles[k][:], scalar=mean_tiles[k][:, 0:1], in1=gain[:], op0=ALU.add, op1=ALU.mult,
+            )
+            u_tiles[k] = u
+
+        def deviation_round(rnd):
+            sum_sq = stats.tile([P, ROUND], F32)
+            for k in tiles_of(rnd):
+                squares = scratch.tile([P, D_MODEL], F32)
+                nc.scalar.activation(
+                    out=squares[:], in_=z_tiles[k][:], func=ACT.Square, bias=mean_tiles[k][:, 0:1], scale=1.0,
+                    accum_out=sum_sq[:, k % ROUND : k % ROUND + 1],
+                )
+            sigma = stats.tile([P, ROUND], F32)
+            nc.scalar.activation(out=sigma[:], in_=sum_sq[:], func=ACT.Sqrt, scale=1.0 / (D_MODEL - 1))
+            sigma_eps = stats.tile([P, ROUND], F32)
+            nc.scalar.activation(out=sigma_eps[:], in_=sigma[:], func=ACT.Identity, bias=EPS, scale=1.0)
+            sigma_tiles[rnd] = sigma_eps
+
+        def invert_round(rnd):
+            inv = stats.tile([P, ROUND], F32)
+            nc.vector.reciprocal(out=inv[:], in_=sigma_tiles[rnd][:])
+            inv_tiles[rnd] = inv
+
+        def finish_round(rnd):
+            o = result.tile([P, ROUND, D_MODEL], F32)
+            for k in tiles_of(rnd):
+                j = k % ROUND
+                nc.vector.scalar_tensor_tensor(
+                    out=o[:, j, :], in0=u_tiles[k][:], scalar=inv_tiles[rnd][:, j : j + 1], in1=shift[:],
+                    op0=ALU.mult, op1=ALU.add,
+                )
+            k0 = rnd * ROUND
+            nc.sync.dma_start(out=out_view[:, k0 : k0 + ROUND, :], in_=o[:])
+
+        def live(rnd):
+            return 0 <= rnd < N_ROUNDS
+
+        for step in range(N_ROUNDS + 5):
+            if step % ROUNDS_PER_CHUNK == 0:
+                c = step // ROUNDS_PER_CHUNK
+                if c + CHUNKS_AHEAD < N_CHUNKS:
+                    load_x(c + CHUNKS_AHEAD)
+                if c < N_CHUNKS:
+                    load_residual(c)
+            if live(step - 4):
+                invert_round(step - 4)
+            if live(step - 3):
+                for k in tiles_of(step - 3):
+                    add_residual(k)
+            if live(step):
+                transpose_round(step)
+            if live(step - 3):
+                for k in tiles_of(step - 3):
+                    mean(k)
+                deviation_round(step - 3)
+            if live(step - 4):
+                finish_round(step - 4)
+            if live(step - 3):
+                for k in tiles_of(step - 3):
+                    centre_and_gain(k)
+            if live(step - 1):
+                for k in tiles_of(step - 1):
+                    quantise(k)
+            if live(step - 2):
+                multiply_round(step - 2)

@@ -17,19 +17,16 @@ PACK = 4
 HEADS = 16
 TOKENS = 4096
 D_V = 128
+HALF = D_V // 2
 D_CONTENT = 512
 D_POS = 128
 D_MODEL = D_CONTENT + D_POS
 EPS = 1e-3
 
 N_TILES = TOKENS // P
-QUADS = 4
-HEADS_IN_QUAD = HEADS // QUADS
-HALF_ROWS = 16
-HEAD_ROWS = 2 * HALF_ROWS
-WORDS = HEADS * D_V // 2
-QUAD_WORDS = WORDS // QUADS
-BANKS = 2
+HALVES = 2
+PASSES = 2
+PASS_WORDS = P * PACK // 2
 ROUND = 2
 N_ROUNDS = N_TILES // ROUND
 CHUNK = 4
@@ -37,12 +34,12 @@ N_CHUNKS = N_TILES // CHUNK
 ROUNDS_PER_CHUNK = CHUNK // ROUND
 CHUNKS_AHEAD = 2
 
-FLOPS = 2 * TOKENS * (HEADS * D_V // 2) * D_MODEL
+FLOPS = 2 * TOKENS * (HEADS * HALF) * D_MODEL
 
 
 def tile_multiheadattention_pa_t_kernel(tc, attn_out, inp, w_proj1, w_proj2, ln_a, ln_b, out):
     nc = tc.nc
-    x_view = attn_out.rearrange("h b l f -> h (b l) f").rearrange("h (m k) f -> k m h f", k=N_TILES)
+    x_view = attn_out.rearrange("h b l f -> h (b l) f").rearrange("h (m k) (e j) -> k e m h j", k=N_TILES, e=HALVES)
     inp_view = inp.rearrange("(m k) c -> m k c", k=N_TILES)
     out_view = out.rearrange("(m k) c -> m k c", k=N_TILES)
 
@@ -58,7 +55,7 @@ def tile_multiheadattention_pa_t_kernel(tc, attn_out, inp, w_proj1, w_proj2, ln_
         scratch = ctx.enter_context(tc.tile_pool(name="scratch", bufs=2))
         stats = ctx.enter_context(tc.tile_pool(name="stats", bufs=8))
         result = ctx.enter_context(tc.tile_pool(name="result", bufs=3))
-        t_psum = ctx.enter_context(tc.psum_pool(name="t_psum", bufs=BANKS * ROUND))
+        t_psum = ctx.enter_context(tc.psum_pool(name="t_psum", bufs=HALVES * ROUND))
         y1_psum = ctx.enter_context(tc.psum_pool(name="y1_psum", bufs=ROUND))
         y2_psum = ctx.enter_context(tc.psum_pool(name="y2_psum", bufs=2))
 
@@ -66,11 +63,14 @@ def tile_multiheadattention_pa_t_kernel(tc, attn_out, inp, w_proj1, w_proj2, ln_
         res_tiles = {}
 
         def load_x(c):
-            k0 = c * CHUNK
-            x = xin.tile([P, CHUNK, HEADS, D_V], BF16)
-            for j in range(CHUNK):
-                nc.sync.dma_start(out=x[:, j], in_=x_view[k0 + j])
+            x = xin.tile([P, CHUNK, HALVES, HEADS, HALF], BF16, tag="x")
             x_tiles[c] = x
+            for j in range(CHUNK):
+                load_x_tile(c, j)
+
+        def load_x_tile(c, j):
+            for e in range(HALVES):
+                nc.sync.dma_start(out=x_tiles[c][:, j, e], in_=x_view[c * CHUNK + j, e])
 
         def load_residual(c):
             k0 = c * CHUNK
@@ -79,26 +79,25 @@ def tile_multiheadattention_pa_t_kernel(tc, attn_out, inp, w_proj1, w_proj2, ln_
             res_tiles[c] = res
 
         ln_rows = const.tile([P, 2, D_MODEL], BF16)
-        w1_raw = const.tile([P, QUADS, PACK, D_CONTENT], BF16)
-        w2_raw = const.tile([P, QUADS, PACK, D_POS], BF16)
+        w1_raw = const.tile([P, PASSES, PACK, D_CONTENT], BF16)
+        w2_raw = const.tile([P, PASSES, PACK, D_POS], BF16)
         ident = const.tile([P, P], F32)
         make_identity(nc, ident[:])
         nc.vector.memset(ln_rows[:].rearrange("p a n -> p (a n)").bitcast(I32), 0)
-        nc.vector.memset(w2_raw[:].rearrange("p q t n -> p (q t n)").bitcast(I32), 0)
-        nc.vector.memset(w1_raw[:].rearrange("p q t n -> p (q t n)").bitcast(I32), 0)
-        load_x(0)
+        w1_view = w_proj1.rearrange("(a p t) n -> a p (t n)", a=PASSES, t=PACK)
+        w2_view = w_proj2.rearrange("(a p t) n -> p a (t n)", a=PASSES, t=PACK)
+        x0 = xin.tile([P, CHUNK, HALVES, HEADS, HALF], BF16, tag="x")
+        x_tiles[0] = x0
+        load_x_tile(0, 0)
+        nc.sync.dma_start(out=w1_raw[:, 0].rearrange("p t n -> p (t n)"), in_=w1_view[0])
+        load_x_tile(0, 1)
+        nc.sync.dma_start(out=w1_raw[:, 1].rearrange("p t n -> p (t n)"), in_=w1_view[1])
+        nc.sync.dma_start(out=w2_raw[:].rearrange("p a t n -> p a (t n)"), in_=w2_view)
         nc.sync.dma_start(out=ln_rows[0:1, 0, :], in_=ln_a.unsqueeze(0))
         nc.sync.dma_start(out=ln_rows[0:1, 1, :], in_=ln_b.unsqueeze(0))
-        w1_view = w_proj1.rearrange("(q h j t) n -> h j q (t n)", q=QUADS, h=HEADS_IN_QUAD, t=PACK)
-        w2_view = w_proj2.rearrange("(q h j t) n -> h j q (t n)", q=QUADS, h=HEADS_IN_QUAD, t=PACK)
-        for h in range(HEADS_IN_QUAD):
-            p0 = h * HEAD_ROWS
-            nc.sync.dma_start(
-                out=w2_raw[p0 + HALF_ROWS : p0 + HEAD_ROWS].rearrange("p q t n -> p q (t n)"), in_=w2_view[h]
-            )
-        for h in range(HEADS_IN_QUAD):
-            p0 = h * HEAD_ROWS
-            nc.sync.dma_start(out=w1_raw[p0 : p0 + HALF_ROWS].rearrange("p q t n -> p q (t n)"), in_=w1_view[h])
+        load_x_tile(0, 2)
+        load_x_tile(0, 3)
+        load_residual(0)
         load_x(1)
 
         ones = const.tile([P, P], BF16)
@@ -108,33 +107,31 @@ def tile_multiheadattention_pa_t_kernel(tc, attn_out, inp, w_proj1, w_proj2, ln_
         warm_out = const.tile([P, 1], F32)
         nc.scalar.activation(out=warm_out[:], in_=warm[:], func=ACT.Sqrt)
 
-        w1_grouped = const.tile([P, QUADS, D_CONTENT, PACK], BF16, align_bytes=64)
-        w2_grouped = const.tile([P, QUADS, D_POS, PACK], BF16, align_bytes=64)
+        w1_grouped = const.tile([P, PASSES, D_CONTENT, PACK], BF16, align_bytes=64)
+        w2_grouped = const.tile([P, PASSES, D_POS, PACK], BF16, align_bytes=64)
 
-        gain_bank = y1_psum.tile([P, D_CONTENT], F32, tag="y1")
-        nc.tensor.matmul(out=gain_bank[:], lhsT=ones[:], rhs=ln_rows[:, 0, 0:D_CONTENT], start=True, stop=True)
-        shift_bank = y1_psum.tile([P, D_CONTENT], F32, tag="y1")
-        nc.tensor.matmul(out=shift_bank[:], lhsT=ones[:], rhs=ln_rows[:, 1, 0:D_CONTENT], start=True, stop=True)
-        tails_bank = y2_psum.tile([P, 2, D_POS], F32, tag="y2")
-        nc.tensor.matmul(out=tails_bank[:], lhsT=ones[:], rhs=ln_rows[:, :, D_CONTENT:D_MODEL], start=True, stop=True)
         gain = const.tile([P, D_MODEL], F32)
         shift = const.tile([P, D_MODEL], F32)
-        nc.scalar.copy(out=gain[:, 0:D_CONTENT], in_=gain_bank[:])
-        nc.scalar.copy(out=shift[:, 0:D_CONTENT], in_=shift_bank[:])
-        nc.scalar.copy(out=gain[:, D_CONTENT:D_MODEL], in_=tails_bank[:, 0, :])
-        nc.scalar.copy(out=shift[:, D_CONTENT:D_MODEL], in_=tails_bank[:, 1, :])
 
-        w1_codes = const.tile([P, QUADS, D_CONTENT], U32, align_bytes=64)
-        w1_scales = const.tile([P, QUADS, D_CONTENT], U8, align_bytes=64)
-        w2_codes = const.tile([P, QUADS, D_POS], U32, align_bytes=64)
-        w2_scales = const.tile([P, QUADS, D_POS], U8, align_bytes=64)
-        for q in range(QUADS):
-            nc.scalar.copy(out=w2_grouped[:, q], in_=w2_raw[:, q].rearrange("p t n -> p n t"))
-        nc.vector.quantize_mx(
-            out=w2_codes[:].rearrange("p q n -> p (q n)").bitcast(FP8X4),
-            scales=w2_scales[:].rearrange("p q n -> p (q n)"),
-            in_=w2_grouped[:].rearrange("p q n t -> p (q n t)"),
-        )
+        def spread_gain_and_shift():
+            gain_bank = y1_psum.tile([P, D_CONTENT], F32, tag="y1")
+            nc.tensor.matmul(out=gain_bank[:], lhsT=ones[:], rhs=ln_rows[:, 0, 0:D_CONTENT], start=True, stop=True)
+            shift_bank = y1_psum.tile([P, D_CONTENT], F32, tag="y1")
+            nc.tensor.matmul(out=shift_bank[:], lhsT=ones[:], rhs=ln_rows[:, 1, 0:D_CONTENT], start=True, stop=True)
+            tails_bank = y2_psum.tile([P, 2, D_POS], F32, tag="y2")
+            nc.tensor.matmul(out=tails_bank[:], lhsT=ones[:], rhs=ln_rows[:, :, D_CONTENT:D_MODEL], start=True, stop=True)
+            nc.scalar.copy(out=gain[:, 0:D_CONTENT], in_=gain_bank[:])
+            nc.scalar.copy(out=shift[:, 0:D_CONTENT], in_=shift_bank[:])
+            nc.scalar.copy(out=gain[:, D_CONTENT:D_MODEL], in_=tails_bank[:, 0, :])
+            nc.scalar.copy(out=shift[:, D_CONTENT:D_MODEL], in_=tails_bank[:, 1, :])
+
+        w1_codes = const.tile([P, PASSES, D_CONTENT], U32, align_bytes=64)
+        w1_scales = const.tile([P, PASSES, D_CONTENT], U8, align_bytes=64)
+        w2_codes = const.tile([P, PASSES, D_POS], U32, align_bytes=64)
+        w2_scales = const.tile([P, PASSES, D_POS], U8, align_bytes=64)
+        def group_w2():
+            for a in range(PASSES):
+                nc.scalar.copy(out=w2_grouped[:, a], in_=w2_raw[:, a].rearrange("p t n -> p n t"))
 
         def quantise_w1(q):
             nc.vector.quantize_mx(
@@ -143,11 +140,17 @@ def tile_multiheadattention_pa_t_kernel(tc, attn_out, inp, w_proj1, w_proj2, ln_
                 in_=w1_grouped[:, q].rearrange("p n t -> p (n t)"),
             )
 
-        for q in range(QUADS):
+        for q in range(PASSES):
             nc.vector.tensor_copy(out=w1_grouped[:, q], in_=w1_raw[:, q].rearrange("p t n -> p n t"))
             if q > 0:
                 quantise_w1(q - 1)
-        quantise_w1(QUADS - 1)
+        quantise_w1(PASSES - 1)
+        def quantise_w2():
+            nc.vector.quantize_mx(
+                out=w2_codes[:].rearrange("p q n -> p (q n)").bitcast(FP8X4),
+                scales=w2_scales[:].rearrange("p q n -> p (q n)"),
+                in_=w2_grouped[:].rearrange("p q n t -> p (q n t)"),
+            )
 
         xg_tiles = {}
         code_tiles = {}
@@ -165,29 +168,44 @@ def tile_multiheadattention_pa_t_kernel(tc, attn_out, inp, w_proj1, w_proj2, ln_
 
         def transpose_round(rnd):
             for k in tiles_of(rnd):
-                xg = grouped.tile([P, QUADS, P, PACK], BF16, align_bytes=64)
+                xg = grouped.tile([P, HALVES, PASSES, P, PACK], BF16, align_bytes=64)
                 xg_tiles[k] = xg
-                words = x_tiles[k // CHUNK][:, k % CHUNK].rearrange("p h f -> p (h f)").bitcast(F32)
-                xg_words = xg[:].rearrange("p q m t -> p (q m t)").bitcast(F32).rearrange(
-                    "p (b q m u) -> p b q m u", b=BANKS, m=P, u=2
-                )
-                for b in range(BANKS):
-                    bank = t_psum.tile([P, QUADS // BANKS, 2, P], F32)
-                    for i in range(QUADS // BANKS):
-                        w0 = (b * (QUADS // BANKS) + i) * QUAD_WORDS
+                for e in range(HALVES):
+                    words = x_tiles[k // CHUNK][:, k % CHUNK, e].rearrange("p h j -> p (h j)").bitcast(F32)
+                    bank = t_psum.tile([P, PASSES, 2, P], F32)
+                    for a in range(PASSES):
                         for u in range(2):
-                            nc.tensor.transpose(bank[:, i, u, :], words[:, w0 + u : w0 + QUAD_WORDS : 2], ident[:])
-                    nc.scalar.copy(out=xg_words[:, b], in_=bank[:].rearrange("p q u m -> p q m u"))
+                            first = a * PASS_WORDS + u
+                            last = (a + 1) * PASS_WORDS
+                            nc.tensor.transpose(bank[:, a, u, :], words[:, first:last:2], ident[:])
+                    nc.scalar.copy(
+                        out=xg[:, e].rearrange("p a m t -> p (a m t)").bitcast(F32).rearrange(
+                            "p (a m u) -> p a m u", a=PASSES, u=2
+                        ),
+                        in_=bank[:].rearrange("p a u m -> p a m u"),
+                    )
 
         def quantise(k):
-            codes = packed.tile([P, QUADS, P], U32, align_bytes=64)
-            scales = packed.tile([P, QUADS, P], U8, align_bytes=64)
+            codes = packed.tile([P, HALVES, PASSES, P], U32, align_bytes=64)
+            scales = packed.tile([P, HALVES, PASSES, P], U8, align_bytes=64)
             nc.vector.quantize_mx(
-                out=codes[:].rearrange("p q m -> p (q m)").bitcast(FP8X4),
-                scales=scales[:].rearrange("p q m -> p (q m)"),
-                in_=xg_tiles[k][:].rearrange("p q m t -> p (q m t)"),
+                out=codes[:].rearrange("p e a m -> p (e a m)").bitcast(FP8X4),
+                scales=scales[:].rearrange("p e a m -> p (e a m)"),
+                in_=xg_tiles[k][:].rearrange("p e a m t -> p (e a m t)"),
             )
             code_tiles[k] = (codes, scales)
+
+        def multiply(out_bank, x_codes, x_scales, w_codes, w_scales):
+            for a in range(PASSES):
+                nc.tensor.matmul_mx(
+                    out=out_bank,
+                    lhsT=x_codes[:, a, :].bitcast(FP8X4),
+                    lhsT_scale=x_scales[:, a, :],
+                    rhs=w_codes[:, a, :].bitcast(FP8X4),
+                    rhs_scale=w_scales[:, a, :],
+                    start=(a == 0),
+                    stop=(a == PASSES - 1),
+                )
 
         def multiply_round(rnd):
             y2 = y2_psum.tile([P, ROUND, D_POS], F32, tag="y2")
@@ -195,26 +213,8 @@ def tile_multiheadattention_pa_t_kernel(tc, attn_out, inp, w_proj1, w_proj2, ln_
             for k in tiles_of(rnd):
                 codes, scales = code_tiles[k]
                 y1 = y1_psum.tile([P, D_CONTENT], F32, tag="y1")
-                for q in range(QUADS):
-                    nc.tensor.matmul_mx(
-                        out=y1[:],
-                        lhsT=codes[:, q, :].bitcast(FP8X4),
-                        lhsT_scale=scales[:, q, :],
-                        rhs=w1_codes[:, q, :].bitcast(FP8X4),
-                        rhs_scale=w1_scales[:, q, :],
-                        start=(q == 0),
-                        stop=(q == QUADS - 1),
-                    )
-                for q in range(QUADS):
-                    nc.tensor.matmul_mx(
-                        out=y2[:, k % ROUND, :],
-                        lhsT=codes[:, q, :].bitcast(FP8X4),
-                        lhsT_scale=scales[:, q, :],
-                        rhs=w2_codes[:, q, :].bitcast(FP8X4),
-                        rhs_scale=w2_scales[:, q, :],
-                        start=(q == 0),
-                        stop=(q == QUADS - 1),
-                    )
+                multiply(y1[:], codes[:, 0], scales[:, 0], w1_codes, w1_scales)
+                multiply(y2[:, k % ROUND, :], codes[:, 1], scales[:, 1], w2_codes, w2_scales)
                 y1_tiles[k] = y1
 
         def add_residual(k):
@@ -286,7 +286,7 @@ def tile_multiheadattention_pa_t_kernel(tc, attn_out, inp, w_proj1, w_proj2, ln_
                 c = step // ROUNDS_PER_CHUNK
                 if c + CHUNKS_AHEAD < N_CHUNKS:
                     load_x(c + CHUNKS_AHEAD)
-                if c < N_CHUNKS:
+                if 0 < c < N_CHUNKS:
                     load_residual(c)
             if live(step - 4):
                 invert_round(step - 4)
@@ -295,6 +295,10 @@ def tile_multiheadattention_pa_t_kernel(tc, attn_out, inp, w_proj1, w_proj2, ln_
                     add_residual(k)
             if live(step):
                 transpose_round(step)
+            if step == 0:
+                group_w2()
+            if step == 1:
+                spread_gain_and_shift()
             if live(step - 3):
                 for k in tiles_of(step - 3):
                     mean(k)
@@ -304,6 +308,8 @@ def tile_multiheadattention_pa_t_kernel(tc, attn_out, inp, w_proj1, w_proj2, ln_
             if live(step - 3):
                 for k in tiles_of(step - 3):
                     centre_and_gain(k)
+            if step == 1:
+                quantise_w2()
             if live(step - 1):
                 for k in tiles_of(step - 1):
                     quantise(k)

@@ -26,57 +26,55 @@ EPS = 1e-3
 N_TILES = TOKENS // P
 HALVES = 2
 PASSES = 2
-PASS_WORDS = P * PACK // 2
-ROUND = 2
-N_ROUNDS = N_TILES // ROUND
+PAIR = 2
 CHUNK = 4
 N_CHUNKS = N_TILES // CHUNK
-ROUNDS_PER_CHUNK = CHUNK // ROUND
-CHUNKS_AHEAD = 2
+X_AHEAD = 10
+RESIDUAL_AHEAD = 5
+X_PARTS = 2
 
 FLOPS = 2 * TOKENS * (HEADS * HALF) * D_MODEL
 
 
 def tile_multiheadattention_pa_t_kernel(tc, attn_out, inp, w_proj1, w_proj2, ln_a, ln_b, out):
     nc = tc.nc
-    x_view = attn_out.rearrange("h b l f -> h (b l) f").rearrange("h (m k) (e j) -> k e m h j", k=N_TILES, e=HALVES)
+    x_flat = attn_out.rearrange("h b l f -> h (b l) f")
+    x_view = x_flat.rearrange("h (m k) f -> m h k f", k=N_TILES)
     inp_view = inp.rearrange("(m k) c -> m k c", k=N_TILES)
     out_view = out.rearrange("(m k) c -> m k c", k=N_TILES)
 
     with ExitStack() as ctx:
         ctx.enter_context(tc.manual_schedule())
         const = ctx.enter_context(tc.tile_pool(name="const", bufs=1))
-        xin = ctx.enter_context(tc.tile_pool(name="xin", bufs=3))
-        resin = ctx.enter_context(tc.tile_pool(name="resin", bufs=3))
-        grouped = ctx.enter_context(tc.tile_pool(name="grouped", bufs=3 * ROUND))
-        packed = ctx.enter_context(tc.tile_pool(name="packed", bufs=2 * ROUND))
-        zpool = ctx.enter_context(tc.tile_pool(name="zpool", bufs=2 * ROUND))
-        upool = ctx.enter_context(tc.tile_pool(name="upool", bufs=3 * ROUND))
+        xin = ctx.enter_context(tc.tile_pool(name="xin", bufs=4))
+        halved = ctx.enter_context(tc.tile_pool(name="halved", bufs=4))
+        resin = ctx.enter_context(tc.tile_pool(name="resin", bufs=6))
+        grouped = ctx.enter_context(tc.tile_pool(name="grouped", bufs=5))
+        packed = ctx.enter_context(tc.tile_pool(name="packed", bufs=4))
+        zpool = ctx.enter_context(tc.tile_pool(name="zpool", bufs=6))
+        upool = ctx.enter_context(tc.tile_pool(name="upool", bufs=4))
         scratch = ctx.enter_context(tc.tile_pool(name="scratch", bufs=2))
         stats = ctx.enter_context(tc.tile_pool(name="stats", bufs=8))
-        result = ctx.enter_context(tc.tile_pool(name="result", bufs=3))
-        t_psum = ctx.enter_context(tc.psum_pool(name="t_psum", bufs=HALVES * ROUND))
-        y1_psum = ctx.enter_context(tc.psum_pool(name="y1_psum", bufs=ROUND))
+        result = ctx.enter_context(tc.tile_pool(name="result", bufs=4))
+        t_psum = ctx.enter_context(tc.psum_pool(name="t_psum", bufs=4))
+        y1_psum = ctx.enter_context(tc.psum_pool(name="y1_psum", bufs=2))
         y2_psum = ctx.enter_context(tc.psum_pool(name="y2_psum", bufs=2))
 
         x_tiles = {}
         res_tiles = {}
 
-        def load_x(c):
-            x = xin.tile([P, CHUNK, HALVES, HEADS, HALF], BF16, tag="x")
-            x_tiles[c] = x
-            for j in range(CHUNK):
-                load_x_tile(c, j)
-
-        def load_x_tile(c, j):
-            for e in range(HALVES):
-                nc.sync.dma_start(out=x_tiles[c][:, j, e], in_=x_view[c * CHUNK + j, e])
-
-        def load_residual(c):
+        def load_x(c, part):
+            if part == 0:
+                x = xin.tile([P, HEADS, CHUNK, D_V], BF16)
+                x_tiles[c] = x
             k0 = c * CHUNK
-            res = resin.tile([P, CHUNK, D_MODEL], BF16)
-            nc.sync.dma_start(out=res[:], in_=inp_view[:, k0 : k0 + CHUNK, :])
-            res_tiles[c] = res
+            heads = slice(part * HEADS // X_PARTS, (part + 1) * HEADS // X_PARTS)
+            nc.sync.dma_start(out=x_tiles[c][:, heads], in_=x_view[:, heads, k0 : k0 + CHUNK, :])
+
+        def load_residual(p):
+            res = resin.tile([P, PAIR, D_MODEL], BF16)
+            nc.sync.dma_start(out=res[:], in_=inp_view[:, p * PAIR : (p + 1) * PAIR, :])
+            res_tiles[p] = res
 
         ln_rows = const.tile([P, 2, D_MODEL], BF16)
         w1_raw = const.tile([P, PASSES, PACK, D_CONTENT], BF16)
@@ -86,19 +84,18 @@ def tile_multiheadattention_pa_t_kernel(tc, attn_out, inp, w_proj1, w_proj2, ln_
         nc.vector.memset(ln_rows[:].rearrange("p a n -> p (a n)").bitcast(I32), 0)
         w1_view = w_proj1.rearrange("(a p t) n -> a p (t n)", a=PASSES, t=PACK)
         w2_view = w_proj2.rearrange("(a p t) n -> p a (t n)", a=PASSES, t=PACK)
-        x0 = xin.tile([P, CHUNK, HALVES, HEADS, HALF], BF16, tag="x")
-        x_tiles[0] = x0
-        load_x_tile(0, 0)
-        nc.sync.dma_start(out=w1_raw[:, 0].rearrange("p t n -> p (t n)"), in_=w1_view[0])
-        load_x_tile(0, 1)
-        nc.sync.dma_start(out=w1_raw[:, 1].rearrange("p t n -> p (t n)"), in_=w1_view[1])
+        for a in range(PASSES):
+            nc.sync.dma_start(out=w1_raw[:, a].rearrange("p t n -> p (t n)"), in_=w1_view[a])
+        for part in range(X_PARTS):
+            load_x(0, part)
         nc.sync.dma_start(out=w2_raw[:].rearrange("p a t n -> p a (t n)"), in_=w2_view)
+        load_residual(0)
         nc.sync.dma_start(out=ln_rows[0:1, 0, :], in_=ln_a.unsqueeze(0))
         nc.sync.dma_start(out=ln_rows[0:1, 1, :], in_=ln_b.unsqueeze(0))
-        load_x_tile(0, 2)
-        load_x_tile(0, 3)
-        load_residual(0)
-        load_x(1)
+        load_residual(1)
+        for part in range(X_PARTS):
+            load_x(1, part)
+        load_residual(2)
 
         ones = const.tile([P, P], BF16)
         nc.vector.memset(ones[:], 1.0)
@@ -129,6 +126,7 @@ def tile_multiheadattention_pa_t_kernel(tc, attn_out, inp, w_proj1, w_proj2, ln_
         w1_scales = const.tile([P, PASSES, D_CONTENT], U8, align_bytes=64)
         w2_codes = const.tile([P, PASSES, D_POS], U32, align_bytes=64)
         w2_scales = const.tile([P, PASSES, D_POS], U8, align_bytes=64)
+
         def group_w2():
             for a in range(PASSES):
                 nc.scalar.copy(out=w2_grouped[:, a], in_=w2_raw[:, a].rearrange("p t n -> p n t"))
@@ -140,11 +138,9 @@ def tile_multiheadattention_pa_t_kernel(tc, attn_out, inp, w_proj1, w_proj2, ln_
                 in_=w1_grouped[:, q].rearrange("p n t -> p (n t)"),
             )
 
-        for q in range(PASSES):
+        def group_w1(q):
             nc.vector.tensor_copy(out=w1_grouped[:, q], in_=w1_raw[:, q].rearrange("p t n -> p n t"))
-            if q > 0:
-                quantise_w1(q - 1)
-        quantise_w1(PASSES - 1)
+
         def quantise_w2():
             nc.vector.quantize_mx(
                 out=w2_codes[:].rearrange("p q n -> p (q n)").bitcast(FP8X4),
@@ -152,6 +148,7 @@ def tile_multiheadattention_pa_t_kernel(tc, attn_out, inp, w_proj1, w_proj2, ln_
                 in_=w2_grouped[:].rearrange("p q n t -> p (q n t)"),
             )
 
+        xh_tiles = {}
         xg_tiles = {}
         code_tiles = {}
         y1_tiles = {}
@@ -161,29 +158,31 @@ def tile_multiheadattention_pa_t_kernel(tc, attn_out, inp, w_proj1, w_proj2, ln_
         mean_tiles = {}
         u_tiles = {}
         sigma_tiles = {}
-        inv_tiles = {}
 
-        def tiles_of(rnd):
-            return range(rnd * ROUND, (rnd + 1) * ROUND)
+        def split_halves(k):
+            xh = halved.tile([P, HALVES, 2, HEADS * HALF // PACK], F32)
+            x = x_tiles[k // CHUNK][:, :, k % CHUNK, :]
+            copy = nc.vector.tensor_copy if k < CHUNK else nc.scalar.copy
+            copy(
+                out=xh[:].rearrange("p e u (h w) -> p e u h w", h=HEADS),
+                in_=x.bitcast(F32).rearrange("p h (e w u) -> p e u h w", e=HALVES, u=2),
+            )
+            xh_tiles[k] = xh
 
-        def transpose_round(rnd):
-            for k in tiles_of(rnd):
-                xg = grouped.tile([P, HALVES, PASSES, P, PACK], BF16, align_bytes=64)
-                xg_tiles[k] = xg
-                for e in range(HALVES):
-                    words = x_tiles[k // CHUNK][:, k % CHUNK, e].rearrange("p h j -> p (h j)").bitcast(F32)
-                    bank = t_psum.tile([P, PASSES, 2, P], F32)
-                    for a in range(PASSES):
-                        for u in range(2):
-                            first = a * PASS_WORDS + u
-                            last = (a + 1) * PASS_WORDS
-                            nc.tensor.transpose(bank[:, a, u, :], words[:, first:last:2], ident[:])
-                    nc.scalar.copy(
-                        out=xg[:, e].rearrange("p a m t -> p (a m t)").bitcast(F32).rearrange(
-                            "p (a m u) -> p a m u", a=PASSES, u=2
-                        ),
-                        in_=bank[:].rearrange("p a u m -> p a m u"),
-                    )
+        def transpose(k):
+            xg = grouped.tile([P, HALVES, PASSES, P, PACK], BF16, align_bytes=64)
+            xg_tiles[k] = xg
+            for e in range(HALVES):
+                bank = t_psum.tile([P, PASSES, 2, P], F32)
+                for a in range(PASSES):
+                    for u in range(2):
+                        nc.tensor.transpose(bank[:, a, u, :], xh_tiles[k][:, e, u, a * P : (a + 1) * P], ident[:])
+                nc.scalar.copy(
+                    out=xg[:, e].rearrange("p a m t -> p (a m t)").bitcast(F32).rearrange(
+                        "p (a m u) -> p a m u", a=PASSES, u=2
+                    ),
+                    in_=bank[:].rearrange("p a u m -> p a m u"),
+                )
 
         def quantise(k):
             codes = packed.tile([P, HALVES, PASSES, P], U32, align_bytes=64)
@@ -207,37 +206,37 @@ def tile_multiheadattention_pa_t_kernel(tc, attn_out, inp, w_proj1, w_proj2, ln_
                     stop=(a == PASSES - 1),
                 )
 
-        def multiply_round(rnd):
-            y2 = y2_psum.tile([P, ROUND, D_POS], F32, tag="y2")
-            y2_tiles[rnd] = y2
-            for k in tiles_of(rnd):
-                codes, scales = code_tiles[k]
-                y1 = y1_psum.tile([P, D_CONTENT], F32, tag="y1")
-                multiply(y1[:], codes[:, 0], scales[:, 0], w1_codes, w1_scales)
-                multiply(y2[:, k % ROUND, :], codes[:, 1], scales[:, 1], w2_codes, w2_scales)
-                y1_tiles[k] = y1
+        def multiply_tile(k):
+            if k % PAIR == 0:
+                y2 = y2_psum.tile([P, PAIR, D_POS], F32, tag="y2")
+                y2_tiles[k // PAIR] = y2
+            codes, scales = code_tiles[k]
+            y1 = y1_psum.tile([P, D_CONTENT], F32, tag="y1")
+            multiply(y1[:], codes[:, 0], scales[:, 0], w1_codes, w1_scales)
+            multiply(y2_tiles[k // PAIR][:, k % PAIR, :], codes[:, 1], scales[:, 1], w2_codes, w2_scales)
+            y1_tiles[k] = y1
 
         def add_residual(k):
-            res = res_tiles[k // CHUNK]
+            res = res_tiles[k // PAIR]
             z = zpool.tile([P, D_MODEL], F32)
             sums = stats.tile([P, 2], F32)
             nc.vector.scalar_tensor_tensor(
-                out=z[:, 0:D_CONTENT], in0=y1_tiles[k][:], scalar=1.0, in1=res[:, k % CHUNK, 0:D_CONTENT],
+                out=z[:, 0:D_CONTENT], in0=y1_tiles[k][:], scalar=1.0, in1=res[:, k % PAIR, 0:D_CONTENT],
                 op0=ALU.mult, op1=ALU.add, accum_out=sums[:, 0:1],
             )
             nc.vector.scalar_tensor_tensor(
-                out=z[:, D_CONTENT:D_MODEL], in0=y2_tiles[k // ROUND][:, k % ROUND, :], scalar=1.0,
-                in1=res[:, k % CHUNK, D_CONTENT:D_MODEL],
+                out=z[:, D_CONTENT:D_MODEL], in0=y2_tiles[k // PAIR][:, k % PAIR, :], scalar=1.0,
+                in1=res[:, k % PAIR, D_CONTENT:D_MODEL],
                 op0=ALU.mult, op1=ALU.add, accum_out=sums[:, 1:2],
             )
             z_tiles[k] = z
             sums_tiles[k] = sums
 
         def mean(k):
-            scaled_sums = stats.tile([P, 2], F32)
             neg_mean = stats.tile([P, 1], F32)
-            nc.scalar.activation(
-                out=scaled_sums[:], in_=sums_tiles[k][:], func=ACT.Copy, scale=-1.0 / D_MODEL, accum_out=neg_mean[:, 0:1],
+            nc.gpsimd.tensor_scalar(
+                out=neg_mean[:], in0=sums_tiles[k][:, 0:1], scalar1=sums_tiles[k][:, 1:2], scalar2=-1.0 / D_MODEL,
+                op0=ALU.add, op1=ALU.mult,
             )
             mean_tiles[k] = neg_mean
 
@@ -248,70 +247,71 @@ def tile_multiheadattention_pa_t_kernel(tc, attn_out, inp, w_proj1, w_proj2, ln_
             )
             u_tiles[k] = u
 
-        def deviation_round(rnd):
-            sum_sq = stats.tile([P, ROUND], F32)
-            for k in tiles_of(rnd):
+        def deviation_pair(k0):
+            sum_sq = stats.tile([P, PAIR], F32)
+            for k in range(k0, k0 + PAIR):
                 squares = scratch.tile([P, D_MODEL], F32)
                 nc.scalar.activation(
                     out=squares[:], in_=z_tiles[k][:], func=ACT.Square, bias=mean_tiles[k][:, 0:1], scale=1.0,
-                    accum_out=sum_sq[:, k % ROUND : k % ROUND + 1],
+                    accum_out=sum_sq[:, k - k0 : k - k0 + 1],
                 )
-            sigma = stats.tile([P, ROUND], F32)
+            sigma = stats.tile([P, PAIR], F32)
             nc.scalar.activation(out=sigma[:], in_=sum_sq[:], func=ACT.Sqrt, scale=1.0 / (D_MODEL - 1))
-            sigma_eps = stats.tile([P, ROUND], F32)
-            nc.scalar.activation(out=sigma_eps[:], in_=sigma[:], func=ACT.Identity, bias=EPS, scale=1.0)
-            sigma_tiles[rnd] = sigma_eps
+            sigma_eps = stats.tile([P, PAIR], F32)
+            nc.gpsimd.tensor_scalar(out=sigma_eps[:], in0=sigma[:], scalar1=EPS, scalar2=1.0, op0=ALU.add, op1=ALU.mult)
+            sigma_tiles[k0] = sigma_eps
 
-        def invert_round(rnd):
-            inv = stats.tile([P, ROUND], F32)
-            nc.vector.reciprocal(out=inv[:], in_=sigma_tiles[rnd][:])
-            inv_tiles[rnd] = inv
-
-        def finish_round(rnd):
-            o = result.tile([P, ROUND, D_MODEL], F32)
-            for k in tiles_of(rnd):
-                j = k % ROUND
+        def finish_pair(k0):
+            inv = stats.tile([P, PAIR], F32)
+            nc.vector.reciprocal(out=inv[:], in_=sigma_tiles[k0][:])
+            o = result.tile([P, PAIR, D_MODEL], F32)
+            for j in range(PAIR):
                 nc.vector.scalar_tensor_tensor(
-                    out=o[:, j, :], in0=u_tiles[k][:], scalar=inv_tiles[rnd][:, j : j + 1], in1=shift[:],
+                    out=o[:, j, :], in0=u_tiles[k0 + j][:], scalar=inv[:, j : j + 1], in1=shift[:],
                     op0=ALU.mult, op1=ALU.add,
                 )
-            k0 = rnd * ROUND
-            nc.sync.dma_start(out=out_view[:, k0 : k0 + ROUND, :], in_=o[:])
+            nc.sync.dma_start(out=out_view[:, k0 : k0 + PAIR, :], in_=o[:])
 
-        def live(rnd):
-            return 0 <= rnd < N_ROUNDS
+        def live(k):
+            return 0 <= k < N_TILES
 
-        for step in range(N_ROUNDS + 5):
-            if step % ROUNDS_PER_CHUNK == 0:
-                c = step // ROUNDS_PER_CHUNK
-                if c + CHUNKS_AHEAD < N_CHUNKS:
-                    load_x(c + CHUNKS_AHEAD)
-                if 0 < c < N_CHUNKS:
-                    load_residual(c)
-            if live(step - 4):
-                invert_round(step - 4)
-            if live(step - 3):
-                for k in tiles_of(step - 3):
-                    add_residual(k)
+        def ends_pair(k):
+            return live(k) and k % PAIR == PAIR - 1
+
+        for q in range(PASSES):
+            group_w1(q)
+        for q in range(PASSES):
+            quantise_w1(q)
+        for k in range(CHUNK):
+            split_halves(k)
+        for step in range(N_TILES + 5):
+            for c in range(2, N_CHUNKS):
+                for part in range(X_PARTS):
+                    if step == max(0, c * CHUNK - X_AHEAD) + part:
+                        load_x(c, part)
+            for p in range(3, N_TILES // PAIR):
+                if step == p * PAIR - RESIDUAL_AHEAD:
+                    load_residual(p)
             if live(step):
-                transpose_round(step)
+                transpose(step)
             if step == 0:
                 group_w2()
-            if step == 1:
-                spread_gain_and_shift()
-            if live(step - 3):
-                for k in tiles_of(step - 3):
-                    mean(k)
-                deviation_round(step - 3)
-            if live(step - 4):
-                finish_round(step - 4)
-            if live(step - 3):
-                for k in tiles_of(step - 3):
-                    centre_and_gain(k)
+            for k in range(CHUNK, N_TILES):
+                if step == k - (1 if k < 2 * CHUNK else 2):
+                    split_halves(k)
+            if live(step - 2):
+                add_residual(step - 2)
+                mean(step - 2)
             if step == 1:
                 quantise_w2()
             if live(step - 1):
-                for k in tiles_of(step - 1):
-                    quantise(k)
-            if live(step - 2):
-                multiply_round(step - 2)
+                quantise(step - 1)
+                multiply_tile(step - 1)
+            if step == 2:
+                spread_gain_and_shift()
+            if live(step - 3):
+                centre_and_gain(step - 3)
+            if ends_pair(step - 3):
+                deviation_pair(step - 3 - (PAIR - 1))
+            if ends_pair(step - 4):
+                finish_pair(step - 4 - (PAIR - 1))

@@ -51,10 +51,10 @@ def tile_multiheadattention_pa_t_kernel(tc, attn_out, inp, w_proj1, w_proj2, ln_
         resin = ctx.enter_context(tc.tile_pool(name="resin", bufs=6))
         grouped = ctx.enter_context(tc.tile_pool(name="grouped", bufs=5))
         packed = ctx.enter_context(tc.tile_pool(name="packed", bufs=4))
-        zpool = ctx.enter_context(tc.tile_pool(name="zpool", bufs=6))
-        upool = ctx.enter_context(tc.tile_pool(name="upool", bufs=4))
+        zpool = ctx.enter_context(tc.tile_pool(name="zpool", bufs=5))
+        upool = ctx.enter_context(tc.tile_pool(name="upool", bufs=6))
         scratch = ctx.enter_context(tc.tile_pool(name="scratch", bufs=2))
-        stats = ctx.enter_context(tc.tile_pool(name="stats", bufs=8))
+        stats = ctx.enter_context(tc.tile_pool(name="stats", bufs=10))
         result = ctx.enter_context(tc.tile_pool(name="result", bufs=4))
         t_psum = ctx.enter_context(tc.psum_pool(name="t_psum", bufs=4))
         y1_psum = ctx.enter_context(tc.psum_pool(name="y1_psum", bufs=2))
@@ -157,7 +157,10 @@ def tile_multiheadattention_pa_t_kernel(tc, attn_out, inp, w_proj1, w_proj2, ln_
         sums_tiles = {}
         mean_tiles = {}
         u_tiles = {}
+        sum_sq_tiles = {}
         sigma_tiles = {}
+        inv_tiles = {}
+        out_tiles = {}
 
         def split_halves(k):
             xh = halved.tile([P, HALVES, 2, HEADS * HALF // PACK], F32)
@@ -234,7 +237,7 @@ def tile_multiheadattention_pa_t_kernel(tc, attn_out, inp, w_proj1, w_proj2, ln_
 
         def mean(k):
             neg_mean = stats.tile([P, 1], F32)
-            nc.gpsimd.tensor_scalar(
+            nc.vector.tensor_scalar(
                 out=neg_mean[:], in0=sums_tiles[k][:, 0:1], scalar1=sums_tiles[k][:, 1:2], scalar2=-1.0 / D_MODEL,
                 op0=ALU.add, op1=ALU.mult,
             )
@@ -247,36 +250,42 @@ def tile_multiheadattention_pa_t_kernel(tc, attn_out, inp, w_proj1, w_proj2, ln_
             )
             u_tiles[k] = u
 
-        def deviation_pair(k0):
-            sum_sq = stats.tile([P, PAIR], F32)
-            for k in range(k0, k0 + PAIR):
-                squares = scratch.tile([P, D_MODEL], F32)
-                nc.scalar.activation(
-                    out=squares[:], in_=z_tiles[k][:], func=ACT.Square, bias=mean_tiles[k][:, 0:1], scale=1.0,
-                    accum_out=sum_sq[:, k - k0 : k - k0 + 1],
-                )
-            sigma = stats.tile([P, PAIR], F32)
-            nc.scalar.activation(out=sigma[:], in_=sum_sq[:], func=ACT.Sqrt, scale=1.0 / (D_MODEL - 1))
-            sigma_eps = stats.tile([P, PAIR], F32)
-            nc.gpsimd.tensor_scalar(out=sigma_eps[:], in0=sigma[:], scalar1=EPS, scalar2=1.0, op0=ALU.add, op1=ALU.mult)
-            sigma_tiles[k0] = sigma_eps
+        def square(k):
+            if k % PAIR == 0:
+                sum_sq = stats.tile([P, PAIR], F32)
+                sum_sq_tiles[k // PAIR] = sum_sq
+            squares = scratch.tile([P, D_MODEL], F32)
+            nc.scalar.activation(
+                out=squares[:], in_=z_tiles[k][:], func=ACT.Square, bias=mean_tiles[k][:, 0:1], scale=1.0,
+                accum_out=sum_sq_tiles[k // PAIR][:, k % PAIR : k % PAIR + 1],
+            )
 
-        def finish_pair(k0):
+        def deviation(p):
+            sigma = stats.tile([P, PAIR], F32)
+            nc.scalar.activation(out=sigma[:], in_=sum_sq_tiles[p][:], func=ACT.Sqrt, scale=1.0 / (D_MODEL - 1))
+            sigma_eps = stats.tile([P, PAIR], F32)
+            nc.scalar.activation(out=sigma_eps[:], in_=sigma[:], func=ACT.Identity, bias=EPS, scale=1.0)
+            sigma_tiles[p] = sigma_eps
+
+        def invert(p):
             inv = stats.tile([P, PAIR], F32)
-            nc.vector.reciprocal(out=inv[:], in_=sigma_tiles[k0][:])
-            o = result.tile([P, PAIR, D_MODEL], F32)
-            for j in range(PAIR):
-                nc.vector.scalar_tensor_tensor(
-                    out=o[:, j, :], in0=u_tiles[k0 + j][:], scalar=inv[:, j : j + 1], in1=shift[:],
-                    op0=ALU.mult, op1=ALU.add,
-                )
-            nc.sync.dma_start(out=out_view[:, k0 : k0 + PAIR, :], in_=o[:])
+            nc.vector.reciprocal(out=inv[:], in_=sigma_tiles[p][:])
+            inv_tiles[p] = inv
+
+        def finish(k):
+            p, j = divmod(k, PAIR)
+            if j == 0:
+                o = result.tile([P, PAIR, D_MODEL], F32)
+                out_tiles[p] = o
+            nc.vector.scalar_tensor_tensor(
+                out=out_tiles[p][:, j, :], in0=u_tiles[k][:], scalar=inv_tiles[p][:, j : j + 1], in1=shift[:],
+                op0=ALU.mult, op1=ALU.add,
+            )
+            if j == PAIR - 1:
+                nc.sync.dma_start(out=out_view[:, p * PAIR : (p + 1) * PAIR, :], in_=out_tiles[p][:])
 
         def live(k):
             return 0 <= k < N_TILES
-
-        def ends_pair(k):
-            return live(k) and k % PAIR == PAIR - 1
 
         for q in range(PASSES):
             group_w1(q)
@@ -284,7 +293,7 @@ def tile_multiheadattention_pa_t_kernel(tc, attn_out, inp, w_proj1, w_proj2, ln_
             quantise_w1(q)
         for k in range(CHUNK):
             split_halves(k)
-        for step in range(N_TILES + 5):
+        for step in range(N_TILES + 7):
             for c in range(2, N_CHUNKS):
                 for part in range(X_PARTS):
                     if step == max(0, c * CHUNK - X_AHEAD) + part:
@@ -299,19 +308,25 @@ def tile_multiheadattention_pa_t_kernel(tc, attn_out, inp, w_proj1, w_proj2, ln_
             for k in range(CHUNK, N_TILES):
                 if step == k - (1 if k < 2 * CHUNK else 2):
                     split_halves(k)
+            if step == 1:
+                spread_gain_and_shift()
             if live(step - 2):
-                add_residual(step - 2)
-                mean(step - 2)
+                multiply_tile(step - 2)
+            if live(step - 3):
+                add_residual(step - 3)
+            if live(step - 4):
+                square(step - 4)
+                if (step - 4) % PAIR == PAIR - 1:
+                    deviation((step - 4) // PAIR)
             if step == 1:
                 quantise_w2()
             if live(step - 1):
                 quantise(step - 1)
-                multiply_tile(step - 1)
-            if step == 2:
-                spread_gain_and_shift()
             if live(step - 3):
-                centre_and_gain(step - 3)
-            if ends_pair(step - 3):
-                deviation_pair(step - 3 - (PAIR - 1))
-            if ends_pair(step - 4):
-                finish_pair(step - 4 - (PAIR - 1))
+                mean(step - 3)
+            if live(step - 6):
+                if (step - 6) % PAIR == 0:
+                    invert((step - 6) // PAIR)
+                finish(step - 6)
+            if live(step - 4):
+                centre_and_gain(step - 4)

@@ -28,7 +28,8 @@ HALVES = 2
 PASSES = 2
 PAIR = 2
 CHUNK = 4
-N_CHUNKS = N_TILES // CHUNK
+FIRST = 2
+SPLIT = CHUNK - 1
 X_AHEAD = 10
 RESIDUAL_AHEAD = 5
 X_PARTS = 2
@@ -40,6 +41,7 @@ def tile_multiheadattention_pa_t_kernel(tc, attn_out, inp, w_proj1, w_proj2, ln_
     nc = tc.nc
     x_flat = attn_out.rearrange("h b l f -> h (b l) f")
     x_view = x_flat.rearrange("h (m k) f -> m h k f", k=N_TILES)
+    half_view = x_flat.rearrange("h (m k) (e j) -> k e m h j", k=N_TILES, e=HALVES)
     inp_view = inp.rearrange("(m k) c -> m k c", k=N_TILES)
     out_view = out.rearrange("(m k) c -> m k c", k=N_TILES)
 
@@ -48,6 +50,7 @@ def tile_multiheadattention_pa_t_kernel(tc, attn_out, inp, w_proj1, w_proj2, ln_
         const = ctx.enter_context(tc.tile_pool(name="const", bufs=1))
         xin = ctx.enter_context(tc.tile_pool(name="xin", bufs=4))
         halved = ctx.enter_context(tc.tile_pool(name="halved", bufs=4))
+        direct = ctx.enter_context(tc.tile_pool(name="direct", bufs=3))
         resin = ctx.enter_context(tc.tile_pool(name="resin", bufs=6))
         grouped = ctx.enter_context(tc.tile_pool(name="grouped", bufs=5))
         packed = ctx.enter_context(tc.tile_pool(name="packed", bufs=4))
@@ -61,15 +64,24 @@ def tile_multiheadattention_pa_t_kernel(tc, attn_out, inp, w_proj1, w_proj2, ln_
         y2_psum = ctx.enter_context(tc.psum_pool(name="y2_psum", bufs=2))
 
         x_tiles = {}
+        chunk_tiles = {}
+        direct_tiles = {}
         res_tiles = {}
 
-        def load_x(c, part):
+        def load_x(k0, n, part):
             if part == 0:
                 x = xin.tile([P, HEADS, CHUNK, D_V], BF16)
-                x_tiles[c] = x
-            k0 = c * CHUNK
+                for j in range(n):
+                    x_tiles[k0 + j] = x[:, :, j, :]
+                chunk_tiles[k0] = x
             heads = slice(part * HEADS // X_PARTS, (part + 1) * HEADS // X_PARTS)
-            nc.sync.dma_start(out=x_tiles[c][:, heads], in_=x_view[:, heads, k0 : k0 + CHUNK, :])
+            nc.sync.dma_start(out=chunk_tiles[k0][:, heads, 0:n], in_=x_view[:, heads, k0 : k0 + n, :])
+
+        def load_direct(k):
+            xd = direct.tile([P, HALVES, HEADS, HALF], BF16)
+            for e in range(HALVES):
+                nc.sync.dma_start(out=xd[:, e], in_=half_view[k, e])
+            direct_tiles[k] = xd
 
         def load_residual(p):
             res = resin.tile([P, PAIR, D_MODEL], BF16)
@@ -87,15 +99,18 @@ def tile_multiheadattention_pa_t_kernel(tc, attn_out, inp, w_proj1, w_proj2, ln_
         for a in range(PASSES):
             nc.sync.dma_start(out=w1_raw[:, a].rearrange("p t n -> p (t n)"), in_=w1_view[a])
         for part in range(X_PARTS):
-            load_x(0, part)
+            load_x(0, FIRST, part)
         nc.sync.dma_start(out=w2_raw[:].rearrange("p a t n -> p a (t n)"), in_=w2_view)
         load_residual(0)
+        for part in range(X_PARTS):
+            load_x(FIRST, CHUNK - FIRST, part)
         nc.sync.dma_start(out=ln_rows[0:1, 0, :], in_=ln_a.unsqueeze(0))
         nc.sync.dma_start(out=ln_rows[0:1, 1, :], in_=ln_b.unsqueeze(0))
         load_residual(1)
         for part in range(X_PARTS):
-            load_x(1, part)
+            load_x(CHUNK, SPLIT, part)
         load_residual(2)
+        load_direct(CHUNK + SPLIT)
 
         ones = const.tile([P, P], BF16)
         nc.vector.memset(ones[:], 1.0)
@@ -115,12 +130,12 @@ def tile_multiheadattention_pa_t_kernel(tc, attn_out, inp, w_proj1, w_proj2, ln_
             nc.tensor.matmul(out=gain_bank[:], lhsT=ones[:], rhs=ln_rows[:, 0, 0:D_CONTENT], start=True, stop=True)
             shift_bank = y1_psum.tile([P, D_CONTENT], F32, tag="y1")
             nc.tensor.matmul(out=shift_bank[:], lhsT=ones[:], rhs=ln_rows[:, 1, 0:D_CONTENT], start=True, stop=True)
-            tails_bank = y2_psum.tile([P, 2, D_POS], F32, tag="y2")
-            nc.tensor.matmul(out=tails_bank[:], lhsT=ones[:], rhs=ln_rows[:, :, D_CONTENT:D_MODEL], start=True, stop=True)
+            tails_bank = y2_psum.tile([P, D_CONTENT], F32, tag="y2")
+            nc.tensor.matmul(out=tails_bank[:, 0 : 2 * D_POS], lhsT=ones[:], rhs=ln_rows[:, :, D_CONTENT:D_MODEL], start=True, stop=True)
             nc.scalar.copy(out=gain[:, 0:D_CONTENT], in_=gain_bank[:])
             nc.scalar.copy(out=shift[:, 0:D_CONTENT], in_=shift_bank[:])
-            nc.scalar.copy(out=gain[:, D_CONTENT:D_MODEL], in_=tails_bank[:, 0, :])
-            nc.scalar.copy(out=shift[:, D_CONTENT:D_MODEL], in_=tails_bank[:, 1, :])
+            nc.scalar.copy(out=gain[:, D_CONTENT:D_MODEL], in_=tails_bank[:, 0:D_POS])
+            nc.scalar.copy(out=shift[:, D_CONTENT:D_MODEL], in_=tails_bank[:, D_POS : 2 * D_POS])
 
         w1_codes = const.tile([P, PASSES, D_CONTENT], U32, align_bytes=64)
         w1_scales = const.tile([P, PASSES, D_CONTENT], U8, align_bytes=64)
@@ -164,8 +179,8 @@ def tile_multiheadattention_pa_t_kernel(tc, attn_out, inp, w_proj1, w_proj2, ln_
 
         def split_halves(k):
             xh = halved.tile([P, HALVES, 2, HEADS * HALF // PACK], F32)
-            x = x_tiles[k // CHUNK][:, :, k % CHUNK, :]
-            copy = nc.vector.tensor_copy if k < CHUNK else nc.scalar.copy
+            x = x_tiles[k]
+            copy = nc.vector.tensor_copy if k < FIRST else nc.scalar.copy
             copy(
                 out=xh[:].rearrange("p e u (h w) -> p e u h w", h=HEADS),
                 in_=x.bitcast(F32).rearrange("p h (e w u) -> p e u h w", e=HALVES, u=2),
@@ -179,7 +194,12 @@ def tile_multiheadattention_pa_t_kernel(tc, attn_out, inp, w_proj1, w_proj2, ln_
                 bank = t_psum.tile([P, PASSES, 2, P], F32)
                 for a in range(PASSES):
                     for u in range(2):
-                        nc.tensor.transpose(bank[:, a, u, :], xh_tiles[k][:, e, u, a * P : (a + 1) * P], ident[:])
+                        if k in direct_tiles:
+                            words = direct_tiles[k][:, e].rearrange("p h j -> p (h j)").bitcast(F32)
+                            words = words[:, 2 * a * P + u : 2 * (a + 1) * P : 2]
+                        else:
+                            words = xh_tiles[k][:, e, u, a * P : (a + 1) * P]
+                        nc.tensor.transpose(bank[:, a, u, :], words, ident[:])
                 nc.scalar.copy(
                     out=xg[:, e].rearrange("p a m t -> p (a m t)").bitcast(F32).rearrange(
                         "p (a m u) -> p a m u", a=PASSES, u=2
@@ -210,14 +230,13 @@ def tile_multiheadattention_pa_t_kernel(tc, attn_out, inp, w_proj1, w_proj2, ln_
                 )
 
         def multiply_tile(k):
-            if k % PAIR == 0:
-                y2 = y2_psum.tile([P, PAIR, D_POS], F32, tag="y2")
-                y2_tiles[k // PAIR] = y2
             codes, scales = code_tiles[k]
+            y2 = y2_psum.tile([P, D_CONTENT], F32, tag="y2")
             y1 = y1_psum.tile([P, D_CONTENT], F32, tag="y1")
             multiply(y1[:], codes[:, 0], scales[:, 0], w1_codes, w1_scales)
-            multiply(y2_tiles[k // PAIR][:, k % PAIR, :], codes[:, 1], scales[:, 1], w2_codes, w2_scales)
+            multiply(y2[:, 0:D_POS], codes[:, 1], scales[:, 1], w2_codes, w2_scales)
             y1_tiles[k] = y1
+            y2_tiles[k] = y2
 
         def add_residual(k):
             res = res_tiles[k // PAIR]
@@ -228,7 +247,7 @@ def tile_multiheadattention_pa_t_kernel(tc, attn_out, inp, w_proj1, w_proj2, ln_
                 op0=ALU.mult, op1=ALU.add, accum_out=sums[:, 0:1],
             )
             nc.vector.scalar_tensor_tensor(
-                out=z[:, D_CONTENT:D_MODEL], in0=y2_tiles[k // PAIR][:, k % PAIR, :], scalar=1.0,
+                out=z[:, D_CONTENT:D_MODEL], in0=y2_tiles[k][:, 0:D_POS], scalar=1.0,
                 in1=res[:, k % PAIR, D_CONTENT:D_MODEL],
                 op0=ALU.mult, op1=ALU.add, accum_out=sums[:, 1:2],
             )
@@ -291,13 +310,15 @@ def tile_multiheadattention_pa_t_kernel(tc, attn_out, inp, w_proj1, w_proj2, ln_
             group_w1(q)
         for q in range(PASSES):
             quantise_w1(q)
-        for k in range(CHUNK):
+        for k in range(FIRST):
             split_halves(k)
         for step in range(N_TILES + 7):
-            for c in range(2, N_CHUNKS):
+            for k0 in range(2 * CHUNK, N_TILES, CHUNK):
                 for part in range(X_PARTS):
-                    if step == max(0, c * CHUNK - X_AHEAD) + part:
-                        load_x(c, part)
+                    if step == max(0, k0 - X_AHEAD) + part:
+                        load_x(k0, SPLIT, part)
+                if step == max(0, k0 - X_AHEAD) + X_PARTS:
+                    load_direct(k0 + SPLIT)
             for p in range(3, N_TILES // PAIR):
                 if step == p * PAIR - RESIDUAL_AHEAD:
                     load_residual(p)
@@ -305,8 +326,8 @@ def tile_multiheadattention_pa_t_kernel(tc, attn_out, inp, w_proj1, w_proj2, ln_
                 transpose(step)
             if step == 0:
                 group_w2()
-            for k in range(CHUNK, N_TILES):
-                if step == k - (1 if k < 2 * CHUNK else 2):
+            for k in range(FIRST, N_TILES):
+                if step == k - (1 if k < 2 * CHUNK else 2) and k in x_tiles:
                     split_halves(k)
             if step == 1:
                 spread_gain_and_shift()

@@ -29,6 +29,7 @@ PASSES = 2
 PAIR = 2
 CHUNK = 4
 FIRST = 2
+ON_VECTOR = 4
 SPLIT = CHUNK - 1
 X_AHEAD = 10
 RESIDUAL_AHEAD = 5
@@ -101,9 +102,9 @@ def tile_multiheadattention_pa_t_kernel(tc, attn_out, inp, w_proj1, w_proj2, ln_
         for part in range(X_PARTS):
             load_x(0, FIRST, part)
         nc.sync.dma_start(out=w2_raw[:].rearrange("p a t n -> p a (t n)"), in_=w2_view)
-        load_residual(0)
         for part in range(X_PARTS):
             load_x(FIRST, CHUNK - FIRST, part)
+        load_residual(0)
         nc.sync.dma_start(out=ln_rows[0:1, 0, :], in_=ln_a.unsqueeze(0))
         nc.sync.dma_start(out=ln_rows[0:1, 1, :], in_=ln_b.unsqueeze(0))
         load_residual(1)
@@ -144,7 +145,7 @@ def tile_multiheadattention_pa_t_kernel(tc, attn_out, inp, w_proj1, w_proj2, ln_
 
         def group_w2():
             for a in range(PASSES):
-                nc.scalar.copy(out=w2_grouped[:, a], in_=w2_raw[:, a].rearrange("p t n -> p n t"))
+                nc.vector.tensor_copy(out=w2_grouped[:, a], in_=w2_raw[:, a].rearrange("p t n -> p n t"))
 
         def quantise_w1(q):
             nc.vector.quantize_mx(
@@ -180,7 +181,7 @@ def tile_multiheadattention_pa_t_kernel(tc, attn_out, inp, w_proj1, w_proj2, ln_
         def split_halves(k):
             xh = halved.tile([P, HALVES, 2, HEADS * HALF // PACK], F32)
             x = x_tiles[k]
-            copy = nc.vector.tensor_copy if k < FIRST else nc.scalar.copy
+            copy = nc.vector.tensor_copy if k < ON_VECTOR else nc.scalar.copy
             copy(
                 out=xh[:].rearrange("p e u (h w) -> p e u h w", h=HEADS),
                 in_=x.bitcast(F32).rearrange("p h (e w u) -> p e u h w", e=HALVES, u=2),
@@ -255,10 +256,10 @@ def tile_multiheadattention_pa_t_kernel(tc, attn_out, inp, w_proj1, w_proj2, ln_
             sums_tiles[k] = sums
 
         def mean(k):
+            scaled_sums = stats.tile([P, 2], F32)
             neg_mean = stats.tile([P, 1], F32)
-            nc.vector.tensor_scalar(
-                out=neg_mean[:], in0=sums_tiles[k][:, 0:1], scalar1=sums_tiles[k][:, 1:2], scalar2=-1.0 / D_MODEL,
-                op0=ALU.add, op1=ALU.mult,
+            nc.scalar.activation(
+                out=scaled_sums[:], in_=sums_tiles[k][:], func=ACT.Copy, scale=-1.0 / D_MODEL, accum_out=neg_mean[:, 0:1],
             )
             mean_tiles[k] = neg_mean
 
@@ -312,6 +313,8 @@ def tile_multiheadattention_pa_t_kernel(tc, attn_out, inp, w_proj1, w_proj2, ln_
             quantise_w1(q)
         for k in range(FIRST):
             split_halves(k)
+        group_w2()
+        quantise_w2()
         for step in range(N_TILES + 7):
             for k0 in range(2 * CHUNK, N_TILES, CHUNK):
                 for part in range(X_PARTS):
@@ -324,30 +327,25 @@ def tile_multiheadattention_pa_t_kernel(tc, attn_out, inp, w_proj1, w_proj2, ln_
                     load_residual(p)
             if live(step):
                 transpose(step)
-            if step == 0:
-                group_w2()
+            if live(step - 1):
+                quantise(step - 1)
+            if step == 1:
+                spread_gain_and_shift()
             for k in range(FIRST, N_TILES):
                 if step == k - (1 if k < 2 * CHUNK else 2) and k in x_tiles:
                     split_halves(k)
-            if step == 1:
-                spread_gain_and_shift()
             if live(step - 2):
                 multiply_tile(step - 2)
             if live(step - 3):
                 add_residual(step - 3)
+                mean(step - 3)
             if live(step - 4):
                 square(step - 4)
                 if (step - 4) % PAIR == PAIR - 1:
                     deviation((step - 4) // PAIR)
-            if step == 1:
-                quantise_w2()
-            if live(step - 1):
-                quantise(step - 1)
-            if live(step - 3):
-                mean(step - 3)
+            if live(step - 4):
+                centre_and_gain(step - 4)
             if live(step - 6):
                 if (step - 6) % PAIR == 0:
                     invert((step - 6) // PAIR)
                 finish(step - 6)
-            if live(step - 4):
-                centre_and_gain(step - 4)

@@ -29,7 +29,7 @@ PASSES = 2
 PAIR = 2
 CHUNK = 4
 FIRST = 2
-ON_VECTOR = 4
+ON_VECTOR = 6
 SPLIT = CHUNK - 1
 X_AHEAD = 10
 RESIDUAL_AHEAD = 5
@@ -175,6 +175,7 @@ def tile_multiheadattention_pa_t_kernel(tc, attn_out, inp, w_proj1, w_proj2, ln_
         u_tiles = {}
         sum_sq_tiles = {}
         sigma_tiles = {}
+        sigma_eps_tiles = {}
         inv_tiles = {}
         out_tiles = {}
 
@@ -283,13 +284,17 @@ def tile_multiheadattention_pa_t_kernel(tc, attn_out, inp, w_proj1, w_proj2, ln_
         def deviation(p):
             sigma = stats.tile([P, PAIR], F32)
             nc.scalar.activation(out=sigma[:], in_=sum_sq_tiles[p][:], func=ACT.Sqrt, scale=1.0 / (D_MODEL - 1))
+            sigma_tiles[p] = sigma
+
+        def add_eps(p):
+            sigma = sigma_tiles[p]
             sigma_eps = stats.tile([P, PAIR], F32)
             nc.scalar.activation(out=sigma_eps[:], in_=sigma[:], func=ACT.Identity, bias=EPS, scale=1.0)
-            sigma_tiles[p] = sigma_eps
+            sigma_eps_tiles[p] = sigma_eps
 
         def invert(p):
             inv = stats.tile([P, PAIR], F32)
-            nc.vector.reciprocal(out=inv[:], in_=sigma_tiles[p][:])
+            nc.vector.reciprocal(out=inv[:], in_=sigma_eps_tiles[p][:])
             inv_tiles[p] = inv
 
         def finish(k):
@@ -306,6 +311,12 @@ def tile_multiheadattention_pa_t_kernel(tc, attn_out, inp, w_proj1, w_proj2, ln_
 
         def live(k):
             return 0 <= k < N_TILES
+
+        def starts_pair(k):
+            return live(k) and k % PAIR == 0
+
+        def ends_pair(k):
+            return live(k) and k % PAIR == PAIR - 1
 
         for q in range(PASSES):
             group_w1(q)
@@ -327,25 +338,27 @@ def tile_multiheadattention_pa_t_kernel(tc, attn_out, inp, w_proj1, w_proj2, ln_
                     load_residual(p)
             if live(step):
                 transpose(step)
-            if live(step - 1):
-                quantise(step - 1)
             if step == 1:
                 spread_gain_and_shift()
+            if ends_pair(step - 4):
+                add_eps((step - 4) // PAIR)
+            if starts_pair(step - 6):
+                invert((step - 6) // PAIR)
+            if live(step - 1):
+                quantise(step - 1)
+                multiply_tile(step - 1)
             for k in range(FIRST, N_TILES):
                 if step == k - (1 if k < 2 * CHUNK else 2) and k in x_tiles:
                     split_halves(k)
             if live(step - 2):
-                multiply_tile(step - 2)
+                add_residual(step - 2)
             if live(step - 3):
-                add_residual(step - 3)
-                mean(step - 3)
-            if live(step - 4):
-                square(step - 4)
-                if (step - 4) % PAIR == PAIR - 1:
-                    deviation((step - 4) // PAIR)
-            if live(step - 4):
-                centre_and_gain(step - 4)
+                square(step - 3)
+            if live(step - 2):
+                mean(step - 2)
+            if ends_pair(step - 3):
+                deviation((step - 3) // PAIR)
+            if live(step - 3):
+                centre_and_gain(step - 3)
             if live(step - 6):
-                if (step - 6) % PAIR == 0:
-                    invert((step - 6) // PAIR)
                 finish(step - 6)

@@ -30,7 +30,6 @@ PAIR = 2
 CHUNK = 4
 FIRST = 2
 ON_VECTOR = 6
-SPLIT = CHUNK - 1
 X_AHEAD = 10
 RESIDUAL_AHEAD = 5
 X_PARTS = 2
@@ -51,7 +50,7 @@ def tile_multiheadattention_pa_t_kernel(tc, attn_out, inp, w_proj1, w_proj2, ln_
         const = ctx.enter_context(tc.tile_pool(name="const", bufs=1))
         xin = ctx.enter_context(tc.tile_pool(name="xin", bufs=4))
         halved = ctx.enter_context(tc.tile_pool(name="halved", bufs=4))
-        direct = ctx.enter_context(tc.tile_pool(name="direct", bufs=3))
+        direct = ctx.enter_context(tc.tile_pool(name="direct", bufs=4))
         resin = ctx.enter_context(tc.tile_pool(name="resin", bufs=6))
         grouped = ctx.enter_context(tc.tile_pool(name="grouped", bufs=5))
         packed = ctx.enter_context(tc.tile_pool(name="packed", bufs=4))
@@ -68,6 +67,9 @@ def tile_multiheadattention_pa_t_kernel(tc, attn_out, inp, w_proj1, w_proj2, ln_
         chunk_tiles = {}
         direct_tiles = {}
         res_tiles = {}
+
+        def split_count(k0):
+            return CHUNK - 2 if k0 % (2 * CHUNK) == CHUNK and k0 > CHUNK else CHUNK - 1
 
         def load_x(k0, n, part):
             if part == 0:
@@ -109,9 +111,10 @@ def tile_multiheadattention_pa_t_kernel(tc, attn_out, inp, w_proj1, w_proj2, ln_
         nc.sync.dma_start(out=ln_rows[0:1, 1, :], in_=ln_b.unsqueeze(0))
         load_residual(1)
         for part in range(X_PARTS):
-            load_x(CHUNK, SPLIT, part)
+            load_x(CHUNK, split_count(CHUNK), part)
         load_residual(2)
-        load_direct(CHUNK + SPLIT)
+        for k in range(CHUNK + split_count(CHUNK), 2 * CHUNK):
+            load_direct(k)
 
         ones = const.tile([P, P], BF16)
         nc.vector.memset(ones[:], 1.0)
@@ -170,7 +173,6 @@ def tile_multiheadattention_pa_t_kernel(tc, attn_out, inp, w_proj1, w_proj2, ln_
         y1_tiles = {}
         y2_tiles = {}
         z_tiles = {}
-        sums_tiles = {}
         mean_tiles = {}
         u_tiles = {}
         sum_sq_tiles = {}
@@ -242,32 +244,30 @@ def tile_multiheadattention_pa_t_kernel(tc, attn_out, inp, w_proj1, w_proj2, ln_
 
         def add_residual(k):
             res = res_tiles[k // PAIR]
-            z = zpool.tile([P, D_MODEL], F32)
-            sums = stats.tile([P, 2], F32)
+            z = zpool.tile([P, D_MODEL + 1], F32)
             nc.vector.scalar_tensor_tensor(
                 out=z[:, 0:D_CONTENT], in0=y1_tiles[k][:], scalar=1.0, in1=res[:, k % PAIR, 0:D_CONTENT],
-                op0=ALU.mult, op1=ALU.add, accum_out=sums[:, 0:1],
+                op0=ALU.mult, op1=ALU.add, accum_out=z[:, D_MODEL : D_MODEL + 1],
             )
             nc.vector.scalar_tensor_tensor(
                 out=z[:, D_CONTENT:D_MODEL], in0=y2_tiles[k][:, 0:D_POS], scalar=1.0,
                 in1=res[:, k % PAIR, D_CONTENT:D_MODEL],
-                op0=ALU.mult, op1=ALU.add, accum_out=sums[:, 1:2],
+                op0=ALU.mult, op1=ALU.add,
             )
             z_tiles[k] = z
-            sums_tiles[k] = sums
 
         def mean(k):
-            scaled_sums = stats.tile([P, 2], F32)
+            scaled = scratch.tile([P, D_POS + 1], F32)
             neg_mean = stats.tile([P, 1], F32)
             nc.scalar.activation(
-                out=scaled_sums[:], in_=sums_tiles[k][:], func=ACT.Copy, scale=-1.0 / D_MODEL, accum_out=neg_mean[:, 0:1],
+                out=scaled[:], in_=z_tiles[k][:, D_CONTENT : D_MODEL + 1], func=ACT.Copy, scale=-1.0 / D_MODEL, accum_out=neg_mean[:, 0:1],
             )
             mean_tiles[k] = neg_mean
 
         def centre_and_gain(k):
             u = upool.tile([P, D_MODEL], F32)
             nc.vector.scalar_tensor_tensor(
-                out=u[:], in0=z_tiles[k][:], scalar=mean_tiles[k][:, 0:1], in1=gain[:], op0=ALU.add, op1=ALU.mult,
+                out=u[:], in0=z_tiles[k][:, 0:D_MODEL], scalar=mean_tiles[k][:, 0:1], in1=gain[:], op0=ALU.add, op1=ALU.mult,
             )
             u_tiles[k] = u
 
@@ -277,7 +277,7 @@ def tile_multiheadattention_pa_t_kernel(tc, attn_out, inp, w_proj1, w_proj2, ln_
                 sum_sq_tiles[k // PAIR] = sum_sq
             squares = scratch.tile([P, D_MODEL], F32)
             nc.scalar.activation(
-                out=squares[:], in_=z_tiles[k][:], func=ACT.Square, bias=mean_tiles[k][:, 0:1], scale=1.0,
+                out=squares[:], in_=z_tiles[k][:, 0:D_MODEL], func=ACT.Square, bias=mean_tiles[k][:, 0:1], scale=1.0,
                 accum_out=sum_sq_tiles[k // PAIR][:, k % PAIR : k % PAIR + 1],
             )
 
@@ -330,9 +330,10 @@ def tile_multiheadattention_pa_t_kernel(tc, attn_out, inp, w_proj1, w_proj2, ln_
             for k0 in range(2 * CHUNK, N_TILES, CHUNK):
                 for part in range(X_PARTS):
                     if step == max(0, k0 - X_AHEAD) + part:
-                        load_x(k0, SPLIT, part)
-                if step == max(0, k0 - X_AHEAD) + X_PARTS:
-                    load_direct(k0 + SPLIT)
+                        load_x(k0, split_count(k0), part)
+                for k in range(k0 + split_count(k0), k0 + CHUNK):
+                    if step == max(0, k0 - X_AHEAD) + X_PARTS:
+                        load_direct(k)
             for p in range(3, N_TILES // PAIR):
                 if step == p * PAIR - RESIDUAL_AHEAD:
                     load_residual(p)

@@ -30,7 +30,7 @@ PAIR = 2
 CHUNK = 4
 FIRST = 2
 ON_VECTOR = 6
-X_AHEAD = 10
+X_AHEAD = 8
 RESIDUAL_AHEAD = 5
 X_PARTS = 2
 
@@ -237,8 +237,11 @@ def tile_multiheadattention_pa_t_kernel(tc, attn_out, inp, w_proj1, w_proj2, ln_
             codes, scales = code_tiles[k]
             y2 = y2_psum.tile([P, D_CONTENT], F32, tag="y2")
             y1 = y1_psum.tile([P, D_CONTENT], F32, tag="y1")
-            multiply(y1[:], codes[:, 0], scales[:, 0], w1_codes, w1_scales)
+            nc.tensor.matmul(
+                out=y2[:, D_POS:D_CONTENT], lhsT=ones[:], rhs=ln_rows[:, 0, D_POS:D_CONTENT], start=True, stop=True
+            )
             multiply(y2[:, 0:D_POS], codes[:, 1], scales[:, 1], w2_codes, w2_scales)
+            multiply(y1[:], codes[:, 0], scales[:, 0], w1_codes, w1_scales)
             y1_tiles[k] = y1
             y2_tiles[k] = y2
 
@@ -306,7 +309,9 @@ def tile_multiheadattention_pa_t_kernel(tc, attn_out, inp, w_proj1, w_proj2, ln_
                 out=out_tiles[p][:, j, :], in0=u_tiles[k][:], scalar=inv_tiles[p][:, j : j + 1], in1=shift[:],
                 op0=ALU.mult, op1=ALU.add,
             )
-            if j == PAIR - 1:
+            if k >= N_TILES - PAIR:
+                nc.sync.dma_start(out=out_view[:, k, :], in_=out_tiles[p][:, j, :])
+            elif j == PAIR - 1:
                 nc.sync.dma_start(out=out_view[:, p * PAIR : (p + 1) * PAIR, :], in_=out_tiles[p][:])
 
         def live(k):
@@ -318,6 +323,15 @@ def tile_multiheadattention_pa_t_kernel(tc, attn_out, inp, w_proj1, w_proj2, ln_
         def ends_pair(k):
             return live(k) and k % PAIR == PAIR - 1
 
+        def warm_up():
+            warm_bank = y1_psum.tile([P, D_CONTENT], F32, tag="y1")
+            for h in range(HEADS // X_PARTS):
+                nc.tensor.matmul(
+                    out=warm_bank[:, 0 : FIRST * D_V], lhsT=ones[:],
+                    rhs=chunk_tiles[0][:, h, 0:FIRST, :].rearrange("p k f -> p (k f)"), start=True, stop=True,
+                )
+
+        warm_up()
         for q in range(PASSES):
             group_w1(q)
         for q in range(PASSES):

from contextlib import ExitStack

import concourse.mybir as mybir
from concourse.masks import make_identity

BF16 = mybir.dt.bfloat16
F32 = mybir.dt.float32
I32 = mybir.dt.int32
U32 = mybir.dt.uint32
U8 = mybir.dt.uint8
FP8X4 = mybir.dt.float8_e4m3fn_x4
ALU = mybir.AluOpType
ACT = mybir.ActivationFunctionType

P = 128
PACK = 4
HEADS = 16
TOKENS = 4096
D_V = 128
HALF = D_V // 2
D_CONTENT = 512
D_POS = 128
D_MODEL = D_CONTENT + D_POS
EPS = 1e-3

N_TILES = TOKENS // P
HALVES = 2
PASSES = 2
PAIR = 2
CHUNK = 4
FIRST = 2
ON_VECTOR = 6
X_AHEAD = 8
RESIDUAL_AHEAD = 5
X_PARTS = 2

FLOPS = 2 * TOKENS * (HEADS * HALF) * D_MODEL


def tile_multiheadattention_pa_t_kernel(tc, attn_out, inp, w_proj1, w_proj2, ln_a, ln_b, out):
    nc = tc.nc
    x_flat = attn_out.rearrange("h b l f -> h (b l) f")
    x_view = x_flat.rearrange("h (m k) f -> m h k f", k=N_TILES)
    half_view = x_flat.rearrange("h (m k) (e j) -> k e m h j", k=N_TILES, e=HALVES)
    inp_view = inp.rearrange("(m k) c -> m k c", k=N_TILES)
    out_view = out.rearrange("(m k) c -> m k c", k=N_TILES)

    with ExitStack() as ctx:
        ctx.enter_context(tc.manual_schedule())
        const = ctx.enter_context(tc.tile_pool(name="const", bufs=1))
        xin = ctx.enter_context(tc.tile_pool(name="xin", bufs=4))
        halved = ctx.enter_context(tc.tile_pool(name="halved", bufs=4))
        direct = ctx.enter_context(tc.tile_pool(name="direct", bufs=4))
        resin = ctx.enter_context(tc.tile_pool(name="resin", bufs=6))
        grouped = ctx.enter_context(tc.tile_pool(name="grouped", bufs=5))
        packed = ctx.enter_context(tc.tile_pool(name="packed", bufs=4))
        zpool = ctx.enter_context(tc.tile_pool(name="zpool", bufs=5))
        upool = ctx.enter_context(tc.tile_pool(name="upool", bufs=6))
        scratch = ctx.enter_context(tc.tile_pool(name="scratch", bufs=2))
        stats = ctx.enter_context(tc.tile_pool(name="stats", bufs=10))
        result = ctx.enter_context(tc.tile_pool(name="result", bufs=4))
        t_psum = ctx.enter_context(tc.psum_pool(name="t_psum", bufs=4))
        y1_psum = ctx.enter_context(tc.psum_pool(name="y1_psum", bufs=2))
        y2_psum = ctx.enter_context(tc.psum_pool(name="y2_psum", bufs=2))

        x_tiles = {}
        chunk_tiles = {}
        direct_tiles = {}
        res_tiles = {}

        def split_count(k0):
            return CHUNK - 2 if k0 % (2 * CHUNK) == CHUNK and k0 > CHUNK else CHUNK - 1

        def load_x(k0, n, part):
            if part == 0:
                x = xin.tile([P, HEADS, CHUNK, D_V], BF16)
                for j in range(n):
                    x_tiles[k0 + j] = x[:, :, j, :]
                chunk_tiles[k0] = x
            heads = slice(part * HEADS // X_PARTS, (part + 1) * HEADS // X_PARTS)
            nc.sync.dma_start(out=chunk_tiles[k0][:, heads, 0:n], in_=x_view[:, heads, k0 : k0 + n, :])

        def load_direct(k):
            xd = direct.tile([P, HALVES, HEADS, HALF], BF16)
            for e in range(HALVES):
                nc.sync.dma_start(out=xd[:, e], in_=half_view[k, e])
            direct_tiles[k] = xd

        def load_residual(p):
            res = resin.tile([P, PAIR, D_MODEL], BF16)
            nc.sync.dma_start(out=res[:], in_=inp_view[:, p * PAIR : (p + 1) * PAIR, :])
            res_tiles[p] = res

        ln_rows = const.tile([P, 2, D_MODEL], BF16)
        w1_raw = const.tile([P, PASSES, PACK, D_CONTENT], BF16)
        w2_raw = const.tile([P, PASSES, PACK, D_POS], BF16)
        ident = const.tile([P, P], F32)
        make_identity(nc, ident[:])
        nc.vector.memset(ln_rows[:].rearrange("p a n -> p (a n)").bitcast(I32), 0)
        w1_view = w_proj1.rearrange("(a p t) n -> a p (t n)", a=PASSES, t=PACK)
        w2_view = w_proj2.rearrange("(a p t) n -> p a (t n)", a=PASSES, t=PACK)
        for a in range(PASSES):
            nc.sync.dma_start(out=w1_raw[:, a].rearrange("p t n -> p (t n)"), in_=w1_view[a])
        for part in range(X_PARTS):
            load_x(0, FIRST, part)
        nc.sync.dma_start(out=w2_raw[:].rearrange("p a t n -> p a (t n)"), in_=w2_view)
        for part in range(X_PARTS):
            load_x(FIRST, CHUNK - FIRST, part)
        load_residual(0)
        nc.sync.dma_start(out=ln_rows[0:1, 0, :], in_=ln_a.unsqueeze(0))
        nc.sync.dma_start(out=ln_rows[0:1, 1, :], in_=ln_b.unsqueeze(0))
        load_residual(1)
        for part in range(X_PARTS):
            load_x(CHUNK, split_count(CHUNK), part)
        load_residual(2)
        for k in range(CHUNK + split_count(CHUNK), 2 * CHUNK):
            load_direct(k)

        ones = const.tile([P, P], BF16)
        nc.vector.memset(ones[:], 1.0)
        warm = const.tile([P, 1], F32)
        nc.vector.memset(warm[:], 1.0)
        warm_out = const.tile([P, 1], F32)
        nc.scalar.activation(out=warm_out[:], in_=warm[:], func=ACT.Sqrt)

        w1_grouped = const.tile([P, PASSES, D_CONTENT, PACK], BF16, align_bytes=64)
        w2_grouped = const.tile([P, PASSES, D_POS, PACK], BF16, align_bytes=64)

        gain = const.tile([P, D_MODEL], F32)
        shift = const.tile([P, D_MODEL], F32)

        def spread_gain_and_shift():
            gain_bank = y1_psum.tile([P, D_CONTENT], F32, tag="y1")
            nc.tensor.matmul(out=gain_bank[:], lhsT=ones[:], rhs=ln_rows[:, 0, 0:D_CONTENT], start=True, stop=True)
            shift_bank = y1_psum.tile([P, D_CONTENT], F32, tag="y1")
            nc.tensor.matmul(out=shift_bank[:], lhsT=ones[:], rhs=ln_rows[:, 1, 0:D_CONTENT], start=True, stop=True)
            tails_bank = y2_psum.tile([P, D_CONTENT], F32, tag="y2")
            nc.tensor.matmul(out=tails_bank[:, 0 : 2 * D_POS], lhsT=ones[:], rhs=ln_rows[:, :, D_CONTENT:D_MODEL], start=True, stop=True)
            nc.scalar.copy(out=gain[:, 0:D_CONTENT], in_=gain_bank[:])
            nc.scalar.copy(out=shift[:, 0:D_CONTENT], in_=shift_bank[:])
            nc.scalar.copy(out=gain[:, D_CONTENT:D_MODEL], in_=tails_bank[:, 0:D_POS])
            nc.scalar.copy(out=shift[:, D_CONTENT:D_MODEL], in_=tails_bank[:, D_POS : 2 * D_POS])

        w1_codes = const.tile([P, PASSES, D_CONTENT], U32, align_bytes=64)
        w1_scales = const.tile([P, PASSES, D_CONTENT], U8, align_bytes=64)
        w2_codes = const.tile([P, PASSES, D_POS], U32, align_bytes=64)
        w2_scales = const.tile([P, PASSES, D_POS], U8, align_bytes=64)

        def group_w2():
            for a in range(PASSES):
                nc.vector.tensor_copy(out=w2_grouped[:, a], in_=w2_raw[:, a].rearrange("p t n -> p n t"))

        def quantise_w1(q):
            nc.vector.quantize_mx(
                out=w1_codes[:, q, :].bitcast(FP8X4),
                scales=w1_scales[:, q, :],
                in_=w1_grouped[:, q].rearrange("p n t -> p (n t)"),
            )

        def group_w1(q):
            nc.vector.tensor_copy(out=w1_grouped[:, q], in_=w1_raw[:, q].rearrange("p t n -> p n t"))

        def quantise_w2():
            nc.vector.quantize_mx(
                out=w2_codes[:].rearrange("p q n -> p (q n)").bitcast(FP8X4),
                scales=w2_scales[:].rearrange("p q n -> p (q n)"),
                in_=w2_grouped[:].rearrange("p q n t -> p (q n t)"),
            )

        xh_tiles = {}
        xg_tiles = {}
        code_tiles = {}
        y1_tiles = {}
        y2_tiles = {}
        z_tiles = {}
        mean_tiles = {}
        u_tiles = {}
        sum_sq_tiles = {}
        sigma_tiles = {}
        sigma_eps_tiles = {}
        inv_tiles = {}
        out_tiles = {}

        def split_halves(k):
            xh = halved.tile([P, HALVES, 2, HEADS * HALF // PACK], F32)
            x = x_tiles[k]
            copy = nc.vector.tensor_copy if k < ON_VECTOR else nc.scalar.copy
            copy(
                out=xh[:].rearrange("p e u (h w) -> p e u h w", h=HEADS),
                in_=x.bitcast(F32).rearrange("p h (e w u) -> p e u h w", e=HALVES, u=2),
            )
            xh_tiles[k] = xh

        def transpose(k):
            xg = grouped.tile([P, HALVES, PASSES, P, PACK], BF16, align_bytes=64)
            xg_tiles[k] = xg
            for e in range(HALVES):
                bank = t_psum.tile([P, PASSES, 2, P], F32)
                for a in range(PASSES):
                    for u in range(2):
                        if k in direct_tiles:
                            words = direct_tiles[k][:, e].rearrange("p h j -> p (h j)").bitcast(F32)
                            words = words[:, 2 * a * P + u : 2 * (a + 1) * P : 2]
                        else:
                            words = xh_tiles[k][:, e, u, a * P : (a + 1) * P]
                        nc.tensor.transpose(bank[:, a, u, :], words, ident[:])
                nc.scalar.copy(
                    out=xg[:, e].rearrange("p a m t -> p (a m t)").bitcast(F32).rearrange(
                        "p (a m u) -> p a m u", a=PASSES, u=2
                    ),
                    in_=bank[:].rearrange("p a u m -> p a m u"),
                )

        def quantise(k):
            codes = packed.tile([P, HALVES, PASSES, P], U32, align_bytes=64)
            scales = packed.tile([P, HALVES, PASSES, P], U8, align_bytes=64)
            nc.vector.quantize_mx(
                out=codes[:].rearrange("p e a m -> p (e a m)").bitcast(FP8X4),
                scales=scales[:].rearrange("p e a m -> p (e a m)"),
                in_=xg_tiles[k][:].rearrange("p e a m t -> p (e a m t)"),
            )
            code_tiles[k] = (codes, scales)

        def multiply(out_bank, x_codes, x_scales, w_codes, w_scales):
            for a in range(PASSES):
                nc.tensor.matmul_mx(
                    out=out_bank,
                    lhsT=x_codes[:, a, :].bitcast(FP8X4),
                    lhsT_scale=x_scales[:, a, :],
                    rhs=w_codes[:, a, :].bitcast(FP8X4),
                    rhs_scale=w_scales[:, a, :],
                    start=(a == 0),
                    stop=(a == PASSES - 1),
                )

        def multiply_tile(k):
            codes, scales = code_tiles[k]
            y2 = y2_psum.tile([P, D_CONTENT], F32, tag="y2")
            y1 = y1_psum.tile([P, D_CONTENT], F32, tag="y1")
            nc.tensor.matmul(
                out=y2[:, D_POS:D_CONTENT], lhsT=ones[:], rhs=ln_rows[:, 0, D_POS:D_CONTENT], start=True, stop=True
            )
            multiply(y2[:, 0:D_POS], codes[:, 1], scales[:, 1], w2_codes, w2_scales)
            multiply(y1[:], codes[:, 0], scales[:, 0], w1_codes, w1_scales)
            y1_tiles[k] = y1
            y2_tiles[k] = y2

        def add_residual(k):
            res = res_tiles[k // PAIR]
            z = zpool.tile([P, D_MODEL + 1], F32)
            nc.vector.scalar_tensor_tensor(
                out=z[:, 0:D_CONTENT], in0=y1_tiles[k][:], scalar=1.0, in1=res[:, k % PAIR, 0:D_CONTENT],
                op0=ALU.mult, op1=ALU.add, accum_out=z[:, D_MODEL : D_MODEL + 1],
            )
            nc.vector.scalar_tensor_tensor(
                out=z[:, D_CONTENT:D_MODEL], in0=y2_tiles[k][:, 0:D_POS], scalar=1.0,
                in1=res[:, k % PAIR, D_CONTENT:D_MODEL],
                op0=ALU.mult, op1=ALU.add,
            )
            z_tiles[k] = z

        def mean(k):
            scaled = scratch.tile([P, D_POS + 1], F32)
            neg_mean = stats.tile([P, 1], F32)
            nc.scalar.activation(
                out=scaled[:], in_=z_tiles[k][:, D_CONTENT : D_MODEL + 1], func=ACT.Copy, scale=-1.0 / D_MODEL, accum_out=neg_mean[:, 0:1],
            )
            mean_tiles[k] = neg_mean

        def centre_and_gain(k):
            u = upool.tile([P, D_MODEL], F32)
            nc.vector.scalar_tensor_tensor(
                out=u[:], in0=z_tiles[k][:, 0:D_MODEL], scalar=mean_tiles[k][:, 0:1], in1=gain[:], op0=ALU.add, op1=ALU.mult,
            )
            u_tiles[k] = u

        def square(k):
            if k % PAIR == 0:
                sum_sq = stats.tile([P, PAIR], F32)
                sum_sq_tiles[k // PAIR] = sum_sq
            squares = scratch.tile([P, D_MODEL], F32)
            nc.scalar.activation(
                out=squares[:], in_=z_tiles[k][:, 0:D_MODEL], func=ACT.Square, bias=mean_tiles[k][:, 0:1], scale=1.0,
                accum_out=sum_sq_tiles[k // PAIR][:, k % PAIR : k % PAIR + 1],
            )

        def deviation(p):
            sigma = stats.tile([P, PAIR], F32)
            nc.scalar.activation(out=sigma[:], in_=sum_sq_tiles[p][:], func=ACT.Sqrt, scale=1.0 / (D_MODEL - 1))
            sigma_tiles[p] = sigma

        def add_eps(p):
            sigma = sigma_tiles[p]
            sigma_eps = stats.tile([P, PAIR], F32)
            nc.scalar.activation(out=sigma_eps[:], in_=sigma[:], func=ACT.Identity, bias=EPS, scale=1.0)
            sigma_eps_tiles[p] = sigma_eps

        def invert(p):
            inv = stats.tile([P, PAIR], F32)
            nc.vector.reciprocal(out=inv[:], in_=sigma_eps_tiles[p][:])
            inv_tiles[p] = inv

        def finish(k):
            p, j = divmod(k, PAIR)
            if j == 0:
                o = result.tile([P, PAIR, D_MODEL], F32)
                out_tiles[p] = o
            nc.vector.scalar_tensor_tensor(
                out=out_tiles[p][:, j, :], in0=u_tiles[k][:], scalar=inv_tiles[p][:, j : j + 1], in1=shift[:],
                op0=ALU.mult, op1=ALU.add,
            )
            if k >= N_TILES - PAIR:
                nc.sync.dma_start(out=out_view[:, k, :], in_=out_tiles[p][:, j, :])
            elif j == PAIR - 1:
                nc.sync.dma_start(out=out_view[:, p * PAIR : (p + 1) * PAIR, :], in_=out_tiles[p][:])

        def live(k):
            return 0 <= k < N_TILES

        def starts_pair(k):
            return live(k) and k % PAIR == 0

        def ends_pair(k):
            return live(k) and k % PAIR == PAIR - 1

        def warm_up():
            warm_bank = y1_psum.tile([P, D_CONTENT], F32, tag="y1")
            for h in range(HEADS // X_PARTS):
                nc.tensor.matmul(
                    out=warm_bank[:, 0 : FIRST * D_V], lhsT=ones[:],
                    rhs=chunk_tiles[0][:, h, 0:FIRST, :].rearrange("p k f -> p (k f)"), start=True, stop=True,
                )

        warm_up()
        for q in range(PASSES):
            group_w1(q)
        for q in range(PASSES):
            quantise_w1(q)
        for k in range(FIRST):
            split_halves(k)
        group_w2()
        quantise_w2()
        for step in range(N_TILES + 7):
            for k0 in range(2 * CHUNK, N_TILES, CHUNK):
                for part in range(X_PARTS):
                    if step == max(0, k0 - X_AHEAD) + part:
                        load_x(k0, split_count(k0), part)
                for k in range(k0 + split_count(k0), k0 + CHUNK):
                    if step == max(0, k0 - X_AHEAD) + X_PARTS:
                        load_direct(k)
            for p in range(3, N_TILES // PAIR):
                if step == p * PAIR - RESIDUAL_AHEAD:
                    load_residual(p)
            if live(step):
                transpose(step)
            if step == 1:
                spread_gain_and_shift()
            if ends_pair(step - 4):
                add_eps((step - 4) // PAIR)
            if starts_pair(step - 6):
                invert((step - 6) // PAIR)
            if live(step - 1):
                quantise(step - 1)
                multiply_tile(step - 1)
            for k in range(FIRST, N_TILES):
                if step == k - (1 if k < 2 * CHUNK else 2) and k in x_tiles:
                    split_halves(k)
            if live(step - 2):
                add_residual(step - 2)
            if live(step - 3):
                square(step - 3)
            if live(step - 2):
                mean(step - 2)
            if ends_pair(step - 3):
                deviation((step - 3) // PAIR)
            if live(step - 3):
                centre_and_gain(step - 3)
            if live(step - 6):
                finish(step - 6)
